import numpy as np
import ml_dtypes


def mxq(x, axis, fmt="e4m3"):
    dtype, down = {"e4m3": (ml_dtypes.float8_e4m3fn, 7), "e5m2": (ml_dtypes.float8_e5m2, 14)}[fmt]
    v = np.moveaxis(np.asarray(x, np.float32).astype(ml_dtypes.bfloat16).astype(np.float64), axis, -1)
    blocks = v.reshape(v.shape[:-1] + (-1, 32))
    amax = np.abs(blocks).max(-1, keepdims=True)
    byte = np.maximum(np.where(amax > 0, np.frexp(amax)[1] - 1 + 127, 0) - down, 1)
    scale = np.exp2(byte - 127.0)
    codes = (blocks / scale).astype(np.float32).astype(dtype).astype(np.float64)
    return np.moveaxis((codes * scale).reshape(v.shape), -1, axis)


WIDE = False


def mx_kscale(k):
    if not WIDE:
        return np.ones(k)
    levels = np.array([10, -10, 5, -5, 0])
    a = np.random.permutation(np.resize(levels, k // 512 * 4)).reshape(k // 512, 4)
    idx = np.arange(k)
    return np.exp2(a[idx // 512, idx % 128 // 32])


BF16 = ml_dtypes.bfloat16


def bf(x):
    return np.asarray(x, np.float32).astype(BF16)


def f64(x):
    return np.asarray(x).astype(np.float64)


E2M1 = np.array([0.0, 0.5, 1.0, 1.5, 2.0, 3.0, 4.0, 6.0, -0.0, -0.5, -1.0, -1.5, -2.0, -3.0, -4.0, -6.0])


def pack_weight(w, fmt):
    k, n = w.shape
    w = f64(bf(w)).reshape(k // 32, 32, n)
    amax = np.abs(w).max(1)
    if fmt == "e4m3":
        byte = np.frexp(amax)[1] - 1 + 127 - 7
    else:
        mant, ex = np.frexp(amax / 6.0)
        byte = np.where(mant > 0.5, ex, ex - 1) + 127
    byte = np.clip(np.where(amax > 0, byte, 1), 1, 254)
    scaled = (w * np.exp2(127.0 - byte)[:, None, :]).reshape(k, n).astype(np.float32)
    by_word = np.ascontiguousarray(scaled.reshape(k // 512, 128, 4, n).transpose(0, 1, 3, 2))
    if fmt == "e4m3":
        words = by_word.astype(ml_dtypes.float8_e4m3fn).view(np.uint8)
    else:
        c = by_word.astype(ml_dtypes.float4_e2m1fn).view(np.uint8) & 0xF
        words = c[..., 0::2] | (c[..., 1::2] << 4)
    return np.ascontiguousarray(words), np.ascontiguousarray(byte.astype(np.uint8).reshape(k // 512, 16, n))


def unpack_weight(words, scales, fmt):
    g, p, n, _ = words.shape
    if fmt == "e4m3":
        vals = np.ascontiguousarray(words).view(ml_dtypes.float8_e4m3fn).astype(np.float64)
    else:
        nib = np.empty((g, p, n, 4), np.uint8)
        nib[..., 0::2] = words & 0xF
        nib[..., 1::2] = words >> 4
        vals = E2M1[nib]
    vals = vals * np.repeat(np.exp2(scales.astype(np.float64) - 127.0), 8, axis=1)[..., None]
    return vals.transpose(0, 1, 3, 2).reshape(g * 512, n)


N, LQ, LK, DIN, D, H = 32, 64, 64, 512, 512, 8
DH = D // H


def setup_inputs():
    s, t = mx_kscale(DIN), mx_kscale(D)
    c = D ** -0.25
    mask = (np.random.random((N, LQ)) < 0.75).astype(np.float64)
    mask[:, 0] = 1.0
    query_states = bf(np.random.standard_normal((N, LQ, DIN)) * s)
    key_states = bf(np.random.standard_normal((N, LK, DIN)) * s)
    wq = np.random.standard_normal((D, DIN)) * c / np.sqrt(DIN) / s[None, :] * t[:, None]
    Wq_words, Wq_scales = pack_weight(np.ascontiguousarray(wq.T), "e4m3")
    bq = bf(np.random.standard_normal(D) * 0.5 * c * t)
    wk = np.random.standard_normal((D, DIN)) * c / np.sqrt(DIN) / s[None, :] / t[:, None]
    Wk_words, Wk_scales = pack_weight(np.ascontiguousarray(wk.T), "e4m3")
    bk = bf(np.random.standard_normal(D) * 0.5 * c / t)
    logit_scale = bf(np.random.standard_normal(1) * 0.1)
    return {"query_states": query_states,
            "key_states": key_states,
            "attention_mask": bf(mask),
            "Wq_words": Wq_words,
            "Wq_scales": Wq_scales,
            "bq": bq,
            "Wk_words": Wk_words,
            "Wk_scales": Wk_scales,
            "bk": bk,
            "logit_scale": logit_scale}


def reference(query_states, key_states, attention_mask, Wq_words, Wq_scales, bq, Wk_words, Wk_scales, bk, logit_scale):
    n, Lk = key_states.shape[0], key_states.shape[1]
    Lq = query_states.shape[1]
    q = (mxq(f64(query_states), 2, "e4m3") @ unpack_weight(Wq_words, Wq_scales, "e4m3")) + f64(bq)
    k = (mxq(f64(key_states), 2, "e4m3") @ unpack_weight(Wk_words, Wk_scales, "e4m3")) + f64(bk)
    q = q.reshape(n, Lq, H, DH).transpose(0, 2, 1, 3)
    k = k.reshape(n, Lk, H, DH).transpose(0, 2, 1, 3)
    qf = q.transpose(0, 2, 1, 3).reshape(n * Lq, H * DH)
    kf = k.transpose(0, 2, 1, 3).reshape(n * Lk, H * DH)
    logits = (mxq(qf, 1, "e4m3") @ mxq(kf, 1, "e4m3").T).reshape(n, Lq, n, Lk).transpose(0, 2, 1, 3)
    t2v = logits.max(axis=-1)
    v2t = logits.max(axis=-2)
    mask_sum = np.full((n,), float(Lk))
    com_mask_sum = f64(attention_mask).sum(-1)
    t2v = t2v.sum(axis=2) / com_mask_sum[:, None]
    v2t = v2t.sum(axis=2) / mask_sum[None, :]
    r = (t2v + v2t) / 2.0
    r = np.exp(f64(logit_scale)) * r
    return (r, r.T)

@@ -1,0 +1,335 @@
+from contextlib import ExitStack
+
+import concourse.mybir as mybir
+from concourse.masks import make_identity
+
+F32 = mybir.dt.float32
+BF16 = mybir.dt.bfloat16
+I32 = mybir.dt.int32
+U32 = mybir.dt.uint32
+U8 = mybir.dt.uint8
+FP8X4 = mybir.dt.float8_e4m3fn_x4
+ALU = mybir.AluOpType
+ACT = mybir.ActivationFunctionType
+AXIS_X = mybir.AxisListType.X
+
+P = 128
+PACK = 4
+N_SEQ = 32
+SEQ = 64
+FEATURES = 512
+TOKENS = N_SEQ * SEQ
+CHUNK = 512
+N_CHUNKS = TOKENS // CHUNK
+TILES_PER_CHUNK = CHUNK // P
+N_TILES = TOKENS // P
+SEQ_PER_CHUNK = CHUNK // SEQ
+SEQ_PER_TILE = P // SEQ
+SLICES = FEATURES // P
+HALF = CHUNK // 2
+TILES_PER_HALF = HALF // P
+QUERY = 0
+KEY = 1
+LOGIT_BANKS = 4
+PER_SLOT = 5
+HELD_BACK = 1
+
+FLOPS = 2 * 2 * TOKENS * FEATURES * FEATURES + 2 * TOKENS * TOKENS * FEATURES
+
+
+def tile_contraattention_kernel(
+    tc,
+    query_states,
+    key_states,
+    attention_mask,
+    Wq_words,
+    Wq_scales,
+    bq,
+    Wk_words,
+    Wk_scales,
+    bk,
+    logit_scale,
+    out_0,
+    out_1,
+):
+    nc = tc.nc
+    states = (query_states.flatten_outer_dims(), key_states.flatten_outer_dims())
+    weight_words = (Wq_words, Wk_words)
+    weight_scales = (Wq_scales, Wk_scales)
+    biases = (bq, bk)
+
+    with ExitStack() as ctx:
+        ctx.enter_context(tc.manual_schedule())
+        keep = ctx.enter_context(tc.tile_pool(name="keep", bufs=1))
+        stage = ctx.enter_context(tc.tile_pool(name="stage", bufs=4))
+        psum_t = ctx.enter_context(tc.psum_pool(name="psum_t", bufs=2))
+        psum_proj = ctx.enter_context(tc.psum_pool(name="psum_proj", bufs=2))
+        psum_logits = ctx.enter_context(tc.psum_pool(name="psum_logits", bufs=LOGIT_BANKS))
+
+        raw = [
+            [keep.tile([P, TILES_PER_CHUNK, FEATURES], BF16, name="raw_%d_%d" % (s, c)) for c in range(N_CHUNKS)]
+            for s in (QUERY, KEY)
+        ]
+        w_codes = [keep.tile([P, FEATURES], U32, name="w_codes_%d" % s, align_bytes=64) for s in (QUERY, KEY)]
+        w_planes = [keep.tile([P, FEATURES], U8, name="w_planes_%d" % s, align_bytes=64) for s in (QUERY, KEY)]
+        codes = [
+            [keep.tile([P, CHUNK], U32, name="codes_%d_%d" % (s, c), align_bytes=64) for c in range(N_CHUNKS)]
+            for s in (QUERY, KEY)
+        ]
+        planes = [
+            [keep.tile([P, CHUNK], U8, name="planes_%d_%d" % (s, c), align_bytes=64) for c in range(N_CHUNKS)]
+            for s in (QUERY, KEY)
+        ]
+        maxima = [keep.tile([P, 2, N_SEQ], F32, name="maxima_%d" % t) for t in range(N_TILES)]
+
+        ident_f32 = keep.tile([P, P], F32, name="ident_f32")
+        ident_bf16 = keep.tile([P, P], BF16, name="ident_bf16")
+        make_identity(nc, ident_f32[:])
+        make_identity(nc, ident_bf16[:])
+
+        def load_states(s, c):
+            for h in range(2):
+                rows = states[s][c * CHUNK + h * HALF : c * CHUNK + (h + 1) * HALF, :]
+                nc.sync.dma_start(
+                    out=raw[s][c][:, h * TILES_PER_HALF : (h + 1) * TILES_PER_HALF, :],
+                    in_=rows.rearrange("(i p) d -> p i d", p=P),
+                )
+
+        def load_weight(s):
+            rows = weight_scales[s].rearrange("g (b r) n -> (g r) b n", r=PACK)
+            for r in range(PACK):
+                nc.sync.dma_start(out=w_planes[s][r:P:32, :].bitcast(I32), in_=rows[r].bitcast(I32))
+            nc.sync.dma_start(
+                out=w_codes[s][:].bitcast(I32),
+                in_=weight_words[s].rearrange("g p n t -> (g p) (n t)").bitcast(I32),
+            )
+
+        for s in (KEY, QUERY):
+            nc.vector.memset(w_planes[s][:].bitcast(I32), 0)
+        bias_rows = keep.tile([P, P], BF16, name="bias_rows")
+        nc.vector.memset(bias_rows[:], 0.0)
+        mask_sb = keep.tile([P, SEQ], BF16, name="mask_sb")
+        nc.vector.memset(mask_sb[:], 1.0)
+        scale_sb = keep.tile([P, 1], BF16, name="scale_sb")
+
+        nc.sync.dma_start(out=scale_sb[:], in_=logit_scale.partition_broadcast(P))
+        load_states(KEY, 0)
+        load_weight(KEY)
+        for s in (KEY, QUERY):
+            nc.sync.dma_start(
+                out=bias_rows[SLICES * s : SLICES * (s + 1), :],
+                in_=biases[s].rearrange("(j p) -> j p", p=P),
+            )
+        load_states(QUERY, 0)
+        load_weight(QUERY)
+        nc.sync.dma_start(out=mask_sb[0:N_SEQ, :], in_=attention_mask)
+        for c in range(1, N_CHUNKS):
+            load_states(KEY, c)
+            load_states(QUERY, c)
+
+        last_window = SEQ_PER_TILE * (N_TILES - 1)
+        selector = keep.tile([P, last_window + P], F32, name="selector")
+        nc.vector.memset(selector[:], 0.0)
+        for half in range(SEQ_PER_TILE):
+            nc.vector.memset(
+                selector[half * SEQ : (half + 1) * SEQ, last_window + half : last_window + half + 1], 1.0
+            )
+        scaled = keep.tile([P, N_SEQ + P], F32, name="scaled")
+        nc.vector.memset(scaled[:], 0.0)
+        exp_scale = keep.tile([P, 1], F32, name="exp_scale")
+        nc.scalar.activation(out=exp_scale[:], in_=scale_sb[:], func=ACT.Exp)
+        bias_cols = keep.tile([P, 2 * SLICES], F32, name="bias_cols")
+
+        halves = [(s, c, h) for c in range(N_CHUNKS) for s in (KEY, QUERY) for h in range(2)]
+        n_halves = len(halves)
+        in_flight = {}
+
+        def turn(n):
+            s, c, h = halves[n]
+            raw_words = raw[s][c][:].bitcast(F32)
+            turned = psum_t.tile([P, TILES_PER_HALF, 2, P], F32, name="turned", tag="turned")
+            for i in range(TILES_PER_HALF):
+                for u in range(2):
+                    nc.tensor.transpose(
+                        turned[:, i, u, :],
+                        raw_words[:, h * TILES_PER_HALF + i, u : FEATURES // 2 : 2],
+                        ident_f32[:],
+                    )
+            grouped = stage.tile([P, HALF * PACK], BF16, name="grouped", align_bytes=64)
+            nc.scalar.copy(
+                out=grouped[:].bitcast(F32).rearrange("p (i r u) -> p i r u", i=TILES_PER_HALF, u=2),
+                in_=turned[:].rearrange("p i u r -> p i r u"),
+            )
+            in_flight[("grouped", n)] = grouped
+
+        def quantise_states(n):
+            x_codes = stage.tile([P, HALF], U32, name="x_codes", align_bytes=64)
+            x_planes = stage.tile([P, HALF], U8, name="x_planes", align_bytes=64)
+            nc.vector.quantize_mx(
+                out=x_codes[:].bitcast(FP8X4), scales=x_planes[:], in_=in_flight[("grouped", n)][:]
+            )
+            in_flight[("x", n)] = (x_codes, x_planes)
+
+        def project(n):
+            s, c, h = halves[n]
+            x_codes, x_planes = in_flight[("x", n)]
+            by_slice = stage.tile([P, SLICES, HALF], BF16, name="by_slice")
+            for pair in range(SLICES // 2):
+                acc = psum_proj.tile([P, 2, HALF], F32, name="acc", tag="acc")
+                for e in range(2):
+                    cols = slice((2 * pair + e) * P, (2 * pair + e + 1) * P)
+                    nc.tensor.matmul_mx(
+                        out=acc[:, e, :],
+                        lhsT=w_codes[s][:, cols].bitcast(FP8X4),
+                        lhsT_scale=w_planes[s][:, cols],
+                        rhs=x_codes[:].bitcast(FP8X4),
+                        rhs_scale=x_planes[:],
+                        start=True,
+                        stop=True,
+                    )
+                for e in range(2):
+                    j = 2 * pair + e
+                    nc.scalar.activation(
+                        out=by_slice[:, j, :],
+                        in_=acc[:, e, :],
+                        func=ACT.Identity,
+                        bias=bias_cols[:, SLICES * s + j : SLICES * s + j + 1],
+                    )
+            regrouped = stage.tile([P, HALF * PACK], BF16, name="regrouped", align_bytes=64)
+            nc.gpsimd.tensor_scalar(
+                out=regrouped[:].rearrange("p (r j) -> p r j", j=SLICES),
+                in0=by_slice[:].rearrange("p j r -> p r j"),
+                scalar1=1.0,
+                scalar2=0.0,
+                op0=ALU.mult,
+                op1=ALU.add,
+            )
+            in_flight[("regrouped", n)] = regrouped
+
+        def quantise_projected(n):
+            s, c, h = halves[n]
+            cols = slice(h * HALF, (h + 1) * HALF)
+            nc.vector.quantize_mx(
+                out=codes[s][c][:, cols].bitcast(FP8X4),
+                scales=planes[s][c][:, cols],
+                in_=in_flight[("regrouped", n)][:],
+            )
+
+        def unlocked(n):
+            s, c, h = halves[n]
+            other_chunks = c if s == KEY else c + 1
+            first = c * TILES_PER_CHUNK + h * TILES_PER_HALF
+            new = [(s, t, o) for t in range(first, first + TILES_PER_HALF) for o in range(other_chunks)]
+            if h == 1:
+                new.extend([(1 - s, t, c) for t in range(other_chunks * TILES_PER_CHUNK)])
+            return new
+
+        def score(s, t, c):
+            o = 1 - s
+            cols = slice((t % TILES_PER_CHUNK) * P, (t % TILES_PER_CHUNK + 1) * P)
+            logits = psum_logits.tile([P, CHUNK], F32, name="logits")
+            nc.tensor.matmul_mx(
+                out=logits[:],
+                lhsT=codes[s][t // TILES_PER_CHUNK][:, cols].bitcast(FP8X4),
+                lhsT_scale=planes[s][t // TILES_PER_CHUNK][:, cols],
+                rhs=codes[o][c][:].bitcast(FP8X4),
+                rhs_scale=planes[o][c][:],
+                start=True,
+                stop=True,
+            )
+            nc.vector.tensor_reduce(
+                out=maxima[t][:, s, c * SEQ_PER_CHUNK : (c + 1) * SEQ_PER_CHUNK],
+                in_=logits[:].rearrange("p (b m) -> p b m", m=SEQ),
+                axis=AXIS_X,
+                op=ALU.max,
+            )
+
+        turn(0)
+        quantise_states(0)
+        turn(1)
+        quantise_states(1)
+        bias_t = psum_t.tile([P, P], BF16, name="bias_t", tag="turned")
+        nc.tensor.transpose(bias_t[:], bias_rows[:], ident_bf16[:])
+        nc.vector.tensor_copy(out=bias_cols[:], in_=bias_t[:, 0 : 2 * SLICES])
+        project(0)
+        turn(2)
+        quantise_states(2)
+        project(1)
+        waiting = []
+        for n in range(n_halves):
+            if n + 3 < n_halves:
+                turn(n + 3)
+            quantise_projected(n)
+            if n + 3 < n_halves:
+                quantise_states(n + 3)
+            if n + 2 < n_halves:
+                project(n + 2)
+            waiting.extend(unlocked(n))
+            n_now = min(PER_SLOT, max(len(waiting) - HELD_BACK, 0))
+            for unit in waiting[:n_now]:
+                score(*unit)
+            waiting = waiting[n_now:]
+
+        mask_sum = keep.tile([P, 1], F32, name="mask_sum")
+        nc.vector.tensor_reduce(out=mask_sum[:], in_=mask_sb[:], axis=AXIS_X, op=ALU.add)
+        inv_mask_sum = keep.tile([P, 1], F32, name="inv_mask_sum")
+        nc.vector.reciprocal(out=inv_mask_sum[:], in_=mask_sum[:])
+        factors = keep.tile([P, 2, N_SEQ], F32, name="factors")
+        nc.vector.tensor_scalar(
+            out=factors[:, QUERY, :],
+            in0=exp_scale[:].to_broadcast([P, N_SEQ]),
+            scalar1=inv_mask_sum[:, 0:1],
+            scalar2=0.5,
+            op0=ALU.mult,
+            op1=ALU.mult,
+        )
+        nc.vector.tensor_scalar(
+            out=factors[:, KEY, :],
+            in0=exp_scale[:].to_broadcast([P, N_SEQ]),
+            scalar1=0.5 / SEQ,
+            scalar2=None,
+            op0=ALU.mult,
+        )
+
+        n_before = len(waiting) - N_TILES
+        assert waiting[n_before:] == [(KEY, t, N_CHUNKS - 1) for t in range(N_TILES)]
+        for unit in waiting[:n_before]:
+            score(*unit)
+
+        sums = psum_proj.tile([P, 2 * N_SEQ], F32, name="sums", tag="acc")
+
+        def add_up(t):
+            window = last_window - SEQ_PER_TILE * t
+            nc.tensor.matmul(
+                out=sums[:],
+                lhsT=selector[:, window : window + P],
+                rhs=maxima[t][:].rearrange("p s b -> p (s b)"),
+                start=(t == 0),
+                stop=(t == N_TILES - 1),
+            )
+
+        for t in range(N_TILES):
+            score(KEY, t, N_CHUNKS - 1)
+            if t >= LOGIT_BANKS:
+                add_up(t - LOGIT_BANKS)
+        for t in range(N_TILES - LOGIT_BANKS, N_TILES):
+            add_up(t)
+
+        nc.vector.tensor_tensor(
+            out=scaled[:, 0 : 2 * N_SEQ],
+            in0=sums[:],
+            in1=factors[:].rearrange("p s b -> p (s b)"),
+            op=ALU.mult,
+        )
+        flipped = psum_t.tile([P, 2, P], F32, name="flipped", tag="turned")
+        nc.tensor.transpose(flipped[:, QUERY, :], scaled[:, N_SEQ : N_SEQ + P], ident_f32[:])
+        nc.tensor.transpose(flipped[:, KEY, :], scaled[:, 0:P], ident_f32[:])
+        result = keep.tile([P, 2, N_SEQ], F32, name="result")
+        nc.vector.tensor_tensor(
+            out=result[:],
+            in0=scaled[:, 0 : 2 * N_SEQ].rearrange("p (s b) -> p s b", s=2),
+            in1=flipped[:, :, 0:N_SEQ],
+            op=ALU.add,
+        )
+        nc.sync.dma_start(out=out_0, in_=result[0:N_SEQ, QUERY, :])
+        nc.sync.dma_start(out=out_1, in_=result[0:N_SEQ, KEY, :])

@@ -196,14 +196,12 @@ def tile_contraattention_kernel(
                         bias=bias_cols[:, SLICES * s + j : SLICES * s + j + 1],
                     )
             regrouped = stage.tile([P, HALF * PACK], BF16, name="regrouped", align_bytes=64)
-            nc.gpsimd.tensor_scalar(
-                out=regrouped[:].rearrange("p (r j) -> p r j", j=SLICES),
-                in0=by_slice[:].rearrange("p j r -> p r j"),
-                scalar1=1.0,
-                scalar2=0.0,
-                op0=ALU.mult,
-                op1=ALU.add,
-            )
+            regrouped_view = regrouped[:].rearrange("p (g i j) -> p g j i", i=4, j=SLICES)
+            by_slice_view = by_slice[:].rearrange("p j (g i) -> p g j i", i=4)
+            if c == 0:
+                nc.vector.tensor_copy(out=regrouped_view, in_=by_slice_view)
+            else:
+                nc.scalar.copy(out=regrouped_view, in_=by_slice_view)
             in_flight[("regrouped", n)] = regrouped
 
         def quantise_projected(n):

@@ -33,6 +33,8 @@ KEY = 1
 LOGIT_BANKS = 4
 PER_SLOT = 5
 HELD_BACK = 1
+HELP_EVERY = 4
+SUM_LAG = 2 * HELP_EVERY + LOGIT_BANKS
 
 FLOPS = 2 * 2 * TOKENS * FEATURES * FEATURES + 2 * TOKENS * TOKENS * FEATURES
 
@@ -62,6 +64,7 @@ def tile_contraattention_kernel(
         ctx.enter_context(tc.manual_schedule())
         keep = ctx.enter_context(tc.tile_pool(name="keep", bufs=1))
         stage = ctx.enter_context(tc.tile_pool(name="stage", bufs=4))
+        halving = ctx.enter_context(tc.tile_pool(name="halving", bufs=4))
         psum_t = ctx.enter_context(tc.psum_pool(name="psum_t", bufs=2))
         psum_proj = ctx.enter_context(tc.psum_pool(name="psum_proj", bufs=2))
         psum_logits = ctx.enter_context(tc.psum_pool(name="psum_logits", bufs=LOGIT_BANKS))
@@ -222,7 +225,7 @@ def tile_contraattention_kernel(
                 new.extend([(1 - s, t, c) for t in range(other_chunks * TILES_PER_CHUNK)])
             return new
 
-        def score(s, t, c):
+        def multiply(s, t, c):
             o = 1 - s
             cols = slice((t % TILES_PER_CHUNK) * P, (t % TILES_PER_CHUNK + 1) * P)
             logits = psum_logits.tile([P, CHUNK], F32, name="logits")
@@ -235,28 +238,55 @@ def tile_contraattention_kernel(
                 start=True,
                 stop=True,
             )
+            return logits[:].rearrange("p (b m) -> p b m", m=SEQ)
+
+        def largest(s, t, c, candidates):
             nc.vector.tensor_reduce(
                 out=maxima[t][:, s, c * SEQ_PER_CHUNK : (c + 1) * SEQ_PER_CHUNK],
-                in_=logits[:].rearrange("p (b m) -> p b m", m=SEQ),
+                in_=candidates,
                 axis=AXIS_X,
                 op=ALU.max,
             )
 
+        def score(s, t, c):
+            largest(s, t, c, multiply(s, t, c))
+
+        helped = []
+
+        def help_begin(s, t, c):
+            flat = halving.tile([P, SEQ_PER_CHUNK, SEQ], F32, name="flat")
+            nc.scalar.copy(out=flat[:], in_=multiply(s, t, c))
+            larger = halving.tile([P, SEQ_PER_CHUNK, SEQ // 2], F32, name="larger")
+            nc.gpsimd.tensor_tensor(
+                out=larger[:], in0=flat[:, :, 0 : SEQ // 2], in1=flat[:, :, SEQ // 2 : SEQ], op=ALU.subtract
+            )
+            helped.append((s, t, c, flat, larger))
+
+        def help_middle(k):
+            s, t, c, flat, larger = helped[k]
+            nc.scalar.activation(out=larger[:], in_=larger[:], func=ACT.Relu)
+            nc.gpsimd.tensor_tensor(out=larger[:], in0=larger[:], in1=flat[:, :, SEQ // 2 : SEQ], op=ALU.add)
+
+        def help_end(k):
+            s, t, c, flat, larger = helped[k]
+            largest(s, t, c, larger[:])
+
         turn(0)
-        quantise_states(0)
         turn(1)
+        quantise_states(0)
+        turn(2)
         quantise_states(1)
         bias_t = psum_t.tile([P, P], BF16, name="bias_t", tag="turned")
         nc.tensor.transpose(bias_t[:], bias_rows[:], ident_bf16[:])
         nc.vector.tensor_copy(out=bias_cols[:], in_=bias_t[:, 0 : 2 * SLICES])
         project(0)
-        turn(2)
+        turn(3)
         quantise_states(2)
         project(1)
         waiting = []
         for n in range(n_halves):
-            if n + 3 < n_halves:
-                turn(n + 3)
+            if n + 4 < n_halves:
+                turn(n + 4)
             quantise_projected(n)
             if n + 3 < n_halves:
                 quantise_states(n + 3)
@@ -289,11 +319,6 @@ def tile_contraattention_kernel(
             op0=ALU.mult,
         )
 
-        n_before = len(waiting) - N_TILES
-        assert waiting[n_before:] == [(KEY, t, N_CHUNKS - 1) for t in range(N_TILES)]
-        for unit in waiting[:n_before]:
-            score(*unit)
-
         sums = psum_proj.tile([P, 2 * N_SEQ], F32, name="sums", tag="acc")
 
         def add_up(t):
@@ -306,12 +331,26 @@ def tile_contraattention_kernel(
                 stop=(t == N_TILES - 1),
             )
 
+        rest = sorted(waiting, key=lambda unit: unit[1])
+        last_product = {unit[1]: n for n, unit in enumerate(rest)}
+        assert len(last_product) == N_TILES
+        n_helped = len(rest) // HELP_EVERY - 2
+        for n, unit in enumerate(rest):
+            k, phase = divmod(n, HELP_EVERY)
+            if phase == 0 and k < n_helped:
+                help_begin(*unit)
+            else:
+                score(*unit)
+            if phase == 0 and 1 <= k <= n_helped:
+                help_middle(k - 1)
+            if phase == 0 and 2 <= k <= n_helped + 1:
+                help_end(k - 2)
+            for t in range(N_TILES):
+                if last_product[t] + SUM_LAG == n:
+                    add_up(t)
         for t in range(N_TILES):
-            score(KEY, t, N_CHUNKS - 1)
-            if t >= LOGIT_BANKS:
-                add_up(t - LOGIT_BANKS)
-        for t in range(N_TILES - LOGIT_BANKS, N_TILES):
-            add_up(t)
+            if last_product[t] + SUM_LAG >= len(rest):
+                add_up(t)
 
         nc.vector.tensor_tensor(
             out=scaled[:, 0 : 2 * N_SEQ],

@@ -12,6 +12,7 @@ FP8X4 = mybir.dt.float8_e4m3fn_x4
 ALU = mybir.AluOpType
 ACT = mybir.ActivationFunctionType
 AXIS_X = mybir.AxisListType.X
+AXIS_XY = mybir.AxisListType.XY
 
 P = 128
 PACK = 4
@@ -24,17 +25,21 @@ N_CHUNKS = TOKENS // CHUNK
 TILES_PER_CHUNK = CHUNK // P
 N_TILES = TOKENS // P
 SEQ_PER_CHUNK = CHUNK // SEQ
-SEQ_PER_TILE = P // SEQ
 SLICES = FEATURES // P
 HALF = CHUNK // 2
 TILES_PER_HALF = HALF // P
+PAIRS = SEQ // 2
+SEQ_PER_TILE = P // PAIRS
 QUERY = 0
 KEY = 1
 LOGIT_BANKS = 4
-PER_SLOT = 5
+PER_SLOT = 4
 HELD_BACK = 1
-HELP_EVERY = 4
-SUM_LAG = 2 * HELP_EVERY + LOGIT_BANKS
+FIRST_PAIRED = 2
+DIRECT_EVERY = 3
+ALONE_PER_STEPS = (4, 3)
+LAG = 3
+SUM_LAG = 2
 
 FLOPS = 2 * 2 * TOKENS * FEATURES * FEATURES + 2 * TOKENS * TOKENS * FEATURES
 
@@ -64,7 +69,7 @@ def tile_contraattention_kernel(
         ctx.enter_context(tc.manual_schedule())
         keep = ctx.enter_context(tc.tile_pool(name="keep", bufs=1))
         stage = ctx.enter_context(tc.tile_pool(name="stage", bufs=4))
-        halving = ctx.enter_context(tc.tile_pool(name="halving", bufs=4))
+        halving = ctx.enter_context(tc.tile_pool(name="halving", bufs=LAG + 2))
         psum_t = ctx.enter_context(tc.psum_pool(name="psum_t", bufs=2))
         psum_proj = ctx.enter_context(tc.psum_pool(name="psum_proj", bufs=2))
         psum_logits = ctx.enter_context(tc.psum_pool(name="psum_logits", bufs=LOGIT_BANKS))
@@ -75,12 +80,13 @@ def tile_contraattention_kernel(
         ]
         w_codes = [keep.tile([P, FEATURES], U32, name="w_codes_%d" % s, align_bytes=64) for s in (QUERY, KEY)]
         w_planes = [keep.tile([P, FEATURES], U8, name="w_planes_%d" % s, align_bytes=64) for s in (QUERY, KEY)]
+        widths = [CHUNK + (HALF if c >= FIRST_PAIRED else 0) for c in range(N_CHUNKS)]
         codes = [
-            [keep.tile([P, CHUNK], U32, name="codes_%d_%d" % (s, c), align_bytes=64) for c in range(N_CHUNKS)]
+            [keep.tile([P, widths[c]], U32, name="codes_%d_%d" % (s, c), align_bytes=64) for c in range(N_CHUNKS)]
             for s in (QUERY, KEY)
         ]
         planes = [
-            [keep.tile([P, CHUNK], U8, name="planes_%d_%d" % (s, c), align_bytes=64) for c in range(N_CHUNKS)]
+            [keep.tile([P, widths[c]], U8, name="planes_%d_%d" % (s, c), align_bytes=64) for c in range(N_CHUNKS)]
             for s in (QUERY, KEY)
         ]
         maxima = [keep.tile([P, 2, N_SEQ], F32, name="maxima_%d" % t) for t in range(N_TILES)]
@@ -91,11 +97,11 @@ def tile_contraattention_kernel(
         make_identity(nc, ident_bf16[:])
 
         def load_states(s, c):
-            for h in range(2):
-                rows = states[s][c * CHUNK + h * HALF : c * CHUNK + (h + 1) * HALF, :]
+            rows = states[s][c * CHUNK : (c + 1) * CHUNK, :].rearrange("(i p e) d -> e p i d", p=P, e=2)
+            for e in range(2):
                 nc.sync.dma_start(
-                    out=raw[s][c][:, h * TILES_PER_HALF : (h + 1) * TILES_PER_HALF, :],
-                    in_=rows.rearrange("(i p) d -> p i d", p=P),
+                    out=raw[s][c][:, e * TILES_PER_HALF : (e + 1) * TILES_PER_HALF, :],
+                    in_=rows[e],
                 )
 
         def load_weight(s):
@@ -130,12 +136,13 @@ def tile_contraattention_kernel(
             load_states(KEY, c)
             load_states(QUERY, c)
 
-        last_window = SEQ_PER_TILE * (N_TILES - 1)
+        last_window = N_SEQ - SEQ_PER_TILE
         selector = keep.tile([P, last_window + P], F32, name="selector")
         nc.vector.memset(selector[:], 0.0)
-        for half in range(SEQ_PER_TILE):
+        for quarter in range(SEQ_PER_TILE):
             nc.vector.memset(
-                selector[half * SEQ : (half + 1) * SEQ, last_window + half : last_window + half + 1], 1.0
+                selector[quarter * PAIRS : (quarter + 1) * PAIRS, last_window + quarter : last_window + quarter + 1],
+                1.0,
             )
         scaled = keep.tile([P, N_SEQ + P], F32, name="scaled")
         nc.vector.memset(scaled[:], 0.0)
@@ -143,19 +150,23 @@ def tile_contraattention_kernel(
         nc.scalar.activation(out=exp_scale[:], in_=scale_sb[:], func=ACT.Exp)
         bias_cols = keep.tile([P, 2 * SLICES], F32, name="bias_cols")
 
-        halves = [(s, c, h) for c in range(N_CHUNKS) for s in (KEY, QUERY) for h in range(2)]
+        halves = [(s, c, e) for c in range(N_CHUNKS) for s in (KEY, QUERY) for e in range(2)]
         n_halves = len(halves)
         in_flight = {}
 
+        def negated(n):
+            s, c, e = halves[n]
+            return c >= FIRST_PAIRED and e == 1
+
         def turn(n):
-            s, c, h = halves[n]
+            s, c, e = halves[n]
             raw_words = raw[s][c][:].bitcast(F32)
             turned = psum_t.tile([P, TILES_PER_HALF, 2, P], F32, name="turned", tag="turned")
             for i in range(TILES_PER_HALF):
                 for u in range(2):
                     nc.tensor.transpose(
                         turned[:, i, u, :],
-                        raw_words[:, h * TILES_PER_HALF + i, u : FEATURES // 2 : 2],
+                        raw_words[:, e * TILES_PER_HALF + i, u : FEATURES // 2 : 2],
                         ident_f32[:],
                     )
             grouped = stage.tile([P, HALF * PACK], BF16, name="grouped", align_bytes=64)
@@ -174,15 +185,15 @@ def tile_contraattention_kernel(
             in_flight[("x", n)] = (x_codes, x_planes)
 
         def project(n):
-            s, c, h = halves[n]
+            s, c, e = halves[n]
             x_codes, x_planes = in_flight[("x", n)]
             by_slice = stage.tile([P, SLICES, HALF], BF16, name="by_slice")
             for pair in range(SLICES // 2):
                 acc = psum_proj.tile([P, 2, HALF], F32, name="acc", tag="acc")
-                for e in range(2):
-                    cols = slice((2 * pair + e) * P, (2 * pair + e + 1) * P)
+                for f in range(2):
+                    cols = slice((2 * pair + f) * P, (2 * pair + f + 1) * P)
                     nc.tensor.matmul_mx(
-                        out=acc[:, e, :],
+                        out=acc[:, f, :],
                         lhsT=w_codes[s][:, cols].bitcast(FP8X4),
                         lhsT_scale=w_planes[s][:, cols],
                         rhs=x_codes[:].bitcast(FP8X4),
@@ -190,16 +201,17 @@ def tile_contraattention_kernel(
                         start=True,
                         stop=True,
                     )
-                for e in range(2):
-                    j = 2 * pair + e
+                for f in range(2):
+                    j = 2 * pair + f
                     nc.scalar.activation(
                         out=by_slice[:, j, :],
-                        in_=acc[:, e, :],
+                        in_=acc[:, f, :],
                         func=ACT.Identity,
                         bias=bias_cols[:, SLICES * s + j : SLICES * s + j + 1],
                     )
-            regrouped = stage.tile([P, HALF * PACK], BF16, name="regrouped", align_bytes=64)
-            regrouped_view = regrouped[:].rearrange("p (g i j) -> p g j i", i=4, j=SLICES)
+            width = HALF * PACK * (2 if negated(n) else 1)
+            regrouped = stage.tile([P, width], BF16, name="regrouped", align_bytes=64)
+            regrouped_view = regrouped[:, 0 : HALF * PACK].rearrange("p (g i j) -> p g j i", i=4, j=SLICES)
             by_slice_view = by_slice[:].rearrange("p j (g i) -> p g j i", i=4)
             if c == 0:
                 nc.vector.tensor_copy(out=regrouped_view, in_=by_slice_view)
@@ -207,9 +219,19 @@ def tile_contraattention_kernel(
                 nc.scalar.copy(out=regrouped_view, in_=by_slice_view)
             in_flight[("regrouped", n)] = regrouped
 
+        def negate(n):
+            regrouped = in_flight[("regrouped", n)]
+            nc.vector.tensor_scalar(
+                out=regrouped[:, HALF * PACK : 2 * HALF * PACK],
+                in0=regrouped[:, 0 : HALF * PACK],
+                scalar1=-1.0,
+                scalar2=None,
+                op0=ALU.mult,
+            )
+
         def quantise_projected(n):
-            s, c, h = halves[n]
-            cols = slice(h * HALF, (h + 1) * HALF)
+            s, c, e = halves[n]
+            cols = slice(e * HALF, (e + (2 if negated(n) else 1)) * HALF)
             nc.vector.quantize_mx(
                 out=codes[s][c][:, cols].bitcast(FP8X4),
                 scales=planes[s][c][:, cols],
@@ -217,59 +239,121 @@ def tile_contraattention_kernel(
             )
 
         def unlocked(n):
-            s, c, h = halves[n]
+            s, c, e = halves[n]
             other_chunks = c if s == KEY else c + 1
-            first = c * TILES_PER_CHUNK + h * TILES_PER_HALF
+            first = c * TILES_PER_CHUNK + e * TILES_PER_HALF
             new = [(s, t, o) for t in range(first, first + TILES_PER_HALF) for o in range(other_chunks)]
-            if h == 1:
+            if e == 1:
                 new.extend([(1 - s, t, c) for t in range(other_chunks * TILES_PER_CHUNK)])
             return new
 
-        def multiply(s, t, c):
+        def product(out, s, t, c, first, width, start, stop):
             o = 1 - s
             cols = slice((t % TILES_PER_CHUNK) * P, (t % TILES_PER_CHUNK + 1) * P)
-            logits = psum_logits.tile([P, CHUNK], F32, name="logits")
             nc.tensor.matmul_mx(
-                out=logits[:],
+                out=out,
                 lhsT=codes[s][t // TILES_PER_CHUNK][:, cols].bitcast(FP8X4),
                 lhsT_scale=planes[s][t // TILES_PER_CHUNK][:, cols],
-                rhs=codes[o][c][:].bitcast(FP8X4),
-                rhs_scale=planes[o][c][:],
-                start=True,
-                stop=True,
+                rhs=codes[o][c][:, first : first + width].bitcast(FP8X4),
+                rhs_scale=planes[o][c][:, first : first + width],
+                start=start,
+                stop=stop,
             )
-            return logits[:].rearrange("p (b m) -> p b m", m=SEQ)
 
-        def largest(s, t, c, candidates):
+        filled = {}
+        clock = [0]
+
+        def note_maxima(s, t, n_sequences):
+            filled[(s, t)] = [filled.get((s, t), [0, 0])[0] + n_sequences, clock[0]]
+
+        def score(s, t, c):
+            logits = psum_logits.tile([P, CHUNK], F32, name="logits")
+            product(logits[:], s, t, c, 0, CHUNK, True, True)
             nc.vector.tensor_reduce(
                 out=maxima[t][:, s, c * SEQ_PER_CHUNK : (c + 1) * SEQ_PER_CHUNK],
-                in_=candidates,
+                in_=logits[:].rearrange("p (e b m) -> p b e m", e=2, m=PAIRS),
+                axis=AXIS_XY,
+                op=ALU.max,
+            )
+            note_maxima(s, t, SEQ_PER_CHUNK)
+
+        units = []
+        begun = []
+
+        def unit_begin(s, t):
+            difference = psum_t.tile([P, 2, HALF], F32, name="difference", tag="turned")
+            odd = psum_proj.tile([P, 2, HALF], F32, name="odd", tag="acc")
+            for g in range(2):
+                product(difference[:, g, :], s, t, FIRST_PAIRED + g, 0, HALF, True, False)
+                product(difference[:, g, :], s, t, FIRST_PAIRED + g, CHUNK, HALF, False, True)
+            for g in range(2):
+                product(odd[:, g, :], s, t, FIRST_PAIRED + g, HALF, HALF, True, True)
+            larger = halving.tile([P, CHUNK], F32, name="larger")
+            nc.scalar.activation(out=larger[:], in_=difference[:].rearrange("p g n -> p (g n)"), func=ACT.Relu)
+            odd_sb = halving.tile([P, CHUNK], F32, name="odd_sb")
+            nc.scalar.copy(out=odd_sb[:], in_=odd[:].rearrange("p g n -> p (g n)"))
+            units.append((s, t, larger, odd_sb))
+            begun.append(clock[0])
+
+        def unit_middle(k):
+            s, t, larger, odd_sb = units[k]
+            nc.gpsimd.tensor_tensor(out=larger[:], in0=larger[:], in1=odd_sb[:], op=ALU.add)
+
+        def unit_end(k):
+            s, t, larger, odd_sb = units[k]
+            nc.vector.tensor_reduce(
+                out=maxima[t][:, s, FIRST_PAIRED * SEQ_PER_CHUNK : N_SEQ],
+                in_=larger[:].rearrange("p (b m) -> p b m", m=PAIRS),
                 axis=AXIS_X,
                 op=ALU.max,
             )
+            note_maxima(s, t, (N_CHUNKS - FIRST_PAIRED) * SEQ_PER_CHUNK)
 
-        def score(s, t, c):
-            largest(s, t, c, multiply(s, t, c))
+        added = []
+        sums_of = {}
 
-        helped = []
-
-        def help_begin(s, t, c):
-            flat = halving.tile([P, SEQ_PER_CHUNK, SEQ], F32, name="flat")
-            nc.scalar.copy(out=flat[:], in_=multiply(s, t, c))
-            larger = halving.tile([P, SEQ_PER_CHUNK, SEQ // 2], F32, name="larger")
-            nc.gpsimd.tensor_tensor(
-                out=larger[:], in0=flat[:, :, 0 : SEQ // 2], in1=flat[:, :, SEQ // 2 : SEQ], op=ALU.subtract
+        def add_up(t):
+            if len(added) == 0:
+                sums_of[0] = psum_logits.tile([P, 2 * N_SEQ], F32, name="sums", tag="logits")
+            first_seq = (t // TILES_PER_CHUNK) * SEQ_PER_CHUNK + (t % TILES_PER_HALF) * SEQ_PER_TILE
+            window = last_window - first_seq
+            nc.tensor.matmul(
+                out=sums_of[0][:],
+                lhsT=selector[:, window : window + P],
+                rhs=maxima[t][:].rearrange("p s b -> p (s b)"),
+                start=(len(added) == 0),
+                stop=(len(added) == N_TILES - 1),
             )
-            helped.append((s, t, c, flat, larger))
+            added.append(t)
 
-        def help_middle(k):
-            s, t, c, flat, larger = helped[k]
-            nc.scalar.activation(out=larger[:], in_=larger[:], func=ACT.Relu)
-            nc.gpsimd.tensor_tensor(out=larger[:], in0=larger[:], in1=flat[:, :, SEQ // 2 : SEQ], op=ALU.add)
+        waiting = []
+        paired = []
+        n_scored = [0, 0]
 
-        def help_end(k):
-            s, t, c, flat, larger = helped[k]
-            largest(s, t, c, larger[:])
+        def score_waiting(n_products):
+            for unit in waiting[n_scored[0] : n_scored[0] + n_products]:
+                score(*unit)
+            n_scored[0] = min(n_scored[0] + n_products, len(waiting))
+
+        def step():
+            clock[0] += 1
+            if len(units) < len(paired):
+                unit_begin(*paired[len(units)])
+            due = (clock[0] * ALONE_PER_STEPS[0]) // ALONE_PER_STEPS[1] - n_scored[1]
+            before = n_scored[0]
+            score_waiting(due)
+            n_scored[1] += n_scored[0] - before
+            for k in range(len(units)):
+                if begun[k] + 1 == clock[0]:
+                    unit_middle(k)
+                if begun[k] + LAG == clock[0]:
+                    unit_end(k)
+            for t in range(N_TILES):
+                if t not in added and all(
+                    filled.get((s, t), [0, 0])[0] == N_SEQ and filled[(s, t)][1] + SUM_LAG <= clock[0]
+                    for s in (QUERY, KEY)
+                ):
+                    add_up(t)
 
         turn(0)
         turn(1)
@@ -283,21 +367,6 @@ def tile_contraattention_kernel(
         turn(3)
         quantise_states(2)
         project(1)
-        waiting = []
-        for n in range(n_halves):
-            if n + 4 < n_halves:
-                turn(n + 4)
-            quantise_projected(n)
-            if n + 3 < n_halves:
-                quantise_states(n + 3)
-            if n + 2 < n_halves:
-                project(n + 2)
-            waiting.extend(unlocked(n))
-            n_now = min(PER_SLOT, max(len(waiting) - HELD_BACK, 0))
-            for unit in waiting[:n_now]:
-                score(*unit)
-            waiting = waiting[n_now:]
-
         mask_sum = keep.tile([P, 1], F32, name="mask_sum")
         nc.vector.tensor_reduce(out=mask_sum[:], in_=mask_sb[:], axis=AXIS_X, op=ALU.add)
         inv_mask_sum = keep.tile([P, 1], F32, name="inv_mask_sum")
@@ -319,38 +388,34 @@ def tile_contraattention_kernel(
             op0=ALU.mult,
         )
 
-        sums = psum_proj.tile([P, 2 * N_SEQ], F32, name="sums", tag="acc")
+        late = []
+        for n in range(n_halves):
+            if n + 4 < n_halves:
+                turn(n + 4)
+            if negated(n):
+                negate(n)
+            if n + 3 < n_halves:
+                quantise_states(n + 3)
+            elif negated(n):
+                score_waiting(1)
+            quantise_projected(n)
+            if n + 2 < n_halves:
+                project(n + 2)
+            for unit in unlocked(n):
+                if unit[2] < FIRST_PAIRED:
+                    waiting.append(unit)
+                elif unit[2] == N_CHUNKS - 1:
+                    late.append((unit[0], unit[1]))
+            score_waiting(min(PER_SLOT, max(len(waiting) - n_scored[0] - HELD_BACK, 0)))
 
-        def add_up(t):
-            window = last_window - SEQ_PER_TILE * t
-            nc.tensor.matmul(
-                out=sums[:],
-                lhsT=selector[:, window : window + P],
-                rhs=maxima[t][:].rearrange("p s b -> p (s b)"),
-                start=(t == 0),
-                stop=(t == N_TILES - 1),
-            )
-
-        rest = sorted(waiting, key=lambda unit: unit[1])
-        last_product = {unit[1]: n for n, unit in enumerate(rest)}
-        assert len(last_product) == N_TILES
-        n_helped = len(rest) // HELP_EVERY - 2
-        for n, unit in enumerate(rest):
-            k, phase = divmod(n, HELP_EVERY)
-            if phase == 0 and k < n_helped:
-                help_begin(*unit)
+        for n, pair in enumerate(sorted(late, key=lambda pair: (QUERY if pair[0] == KEY else KEY, pair[1]))):
+            if n % DIRECT_EVERY == DIRECT_EVERY - 1:
+                waiting.extend([(pair[0], pair[1], c) for c in range(FIRST_PAIRED, N_CHUNKS)])
             else:
-                score(*unit)
-            if phase == 0 and 1 <= k <= n_helped:
-                help_middle(k - 1)
-            if phase == 0 and 2 <= k <= n_helped + 1:
-                help_end(k - 2)
-            for t in range(N_TILES):
-                if last_product[t] + SUM_LAG == n:
-                    add_up(t)
-        for t in range(N_TILES):
-            if last_product[t] + SUM_LAG >= len(rest):
-                add_up(t)
+                paired.append(pair)
+        while len(added) < N_TILES:
+            step()
+        sums = sums_of[0]
 
         nc.vector.tensor_tensor(
             out=scaled[:, 0 : 2 * N_SEQ],

@@ -33,11 +33,15 @@ SEQ_PER_TILE = P // PAIRS
 QUERY = 0
 KEY = 1
 LOGIT_BANKS = 4
-PER_SLOT = 4
+PER_SLOT = 3
 HELD_BACK = 1
 FIRST_PAIRED = 2
-DIRECT_EVERY = 3
+DIRECT_EVERY = 5
 ALONE_PER_STEPS = (4, 3)
+VECTOR_TURNS = ()
+REGROUP_CYCLE = 1
+GPSIMD_SHARE = 1
+REGROUP_BUFS = 1
 LAG = 3
 SUM_LAG = 2
 
@@ -69,6 +73,7 @@ def tile_contraattention_kernel(
         ctx.enter_context(tc.manual_schedule())
         keep = ctx.enter_context(tc.tile_pool(name="keep", bufs=1))
         stage = ctx.enter_context(tc.tile_pool(name="stage", bufs=4))
+        single = ctx.enter_context(tc.tile_pool(name="single", bufs=REGROUP_BUFS))
         halving = ctx.enter_context(tc.tile_pool(name="halving", bufs=LAG + 2))
         psum_t = ctx.enter_context(tc.psum_pool(name="psum_t", bufs=2))
         psum_proj = ctx.enter_context(tc.psum_pool(name="psum_proj", bufs=2))
@@ -170,10 +175,12 @@ def tile_contraattention_kernel(
                         ident_f32[:],
                     )
             grouped = stage.tile([P, HALF * PACK], BF16, name="grouped", align_bytes=64)
-            nc.scalar.copy(
-                out=grouped[:].bitcast(F32).rearrange("p (i r u) -> p i r u", i=TILES_PER_HALF, u=2),
-                in_=turned[:].rearrange("p i u r -> p i r u"),
-            )
+            grouped_view = grouped[:].bitcast(F32).rearrange("p (i r u) -> p i r u", i=TILES_PER_HALF, u=2)
+            turned_view = turned[:].rearrange("p i u r -> p i r u")
+            if n in VECTOR_TURNS:
+                nc.vector.tensor_copy(out=grouped_view, in_=turned_view)
+            else:
+                nc.scalar.copy(out=grouped_view, in_=turned_view)
             in_flight[("grouped", n)] = grouped
 
         def quantise_states(n):
@@ -209,12 +216,26 @@ def tile_contraattention_kernel(
                         func=ACT.Identity,
                         bias=bias_cols[:, SLICES * s + j : SLICES * s + j + 1],
                     )
+            in_flight[("by_slice", n)] = by_slice
+
+        def regroup(n):
+            s, c, e = halves[n]
+            by_slice = in_flight[("by_slice", n)]
             width = HALF * PACK * (2 if negated(n) else 1)
-            regrouped = stage.tile([P, width], BF16, name="regrouped", align_bytes=64)
+            regrouped = single.tile([P, width], BF16, name="regrouped", align_bytes=64)
             regrouped_view = regrouped[:, 0 : HALF * PACK].rearrange("p (g i j) -> p g j i", i=4, j=SLICES)
             by_slice_view = by_slice[:].rearrange("p j (g i) -> p g j i", i=4)
             if c == 0:
                 nc.vector.tensor_copy(out=regrouped_view, in_=by_slice_view)
+            elif n % REGROUP_CYCLE < GPSIMD_SHARE:
+                nc.gpsimd.tensor_scalar(
+                    out=regrouped[:, 0 : HALF * PACK].rearrange("p (r j) -> p r j", j=SLICES),
+                    in0=by_slice[:].rearrange("p j r -> p r j"),
+                    scalar1=1.0,
+                    scalar2=0.0,
+                    op0=ALU.mult,
+                    op1=ALU.add,
+                )
             else:
                 nc.scalar.copy(out=regrouped_view, in_=by_slice_view)
             in_flight[("regrouped", n)] = regrouped
@@ -355,6 +376,19 @@ def tile_contraattention_kernel(
                 ):
                     add_up(t)
 
+        late = []
+
+        def finish(n):
+            quantise_projected(n)
+            for unit in unlocked(n):
+                if unit[2] < FIRST_PAIRED:
+                    waiting.append(unit)
+                elif unit[2] == N_CHUNKS - 1:
+                    late.append((unit[0], unit[1]))
+
+        def score_some():
+            score_waiting(min(PER_SLOT, max(len(waiting) - n_scored[0] - HELD_BACK, 0)))
+
         turn(0)
         turn(1)
         quantise_states(0)
@@ -366,6 +400,7 @@ def tile_contraattention_kernel(
         project(0)
         turn(3)
         quantise_states(2)
+        regroup(0)
         project(1)
         mask_sum = keep.tile([P, 1], F32, name="mask_sum")
         nc.vector.tensor_reduce(out=mask_sum[:], in_=mask_sb[:], axis=AXIS_X, op=ALU.add)
@@ -388,7 +423,6 @@ def tile_contraattention_kernel(
             op0=ALU.mult,
         )
 
-        late = []
         for n in range(n_halves):
             if n + 4 < n_halves:
                 turn(n + 4)
@@ -398,15 +432,12 @@ def tile_contraattention_kernel(
                 quantise_states(n + 3)
             elif negated(n):
                 score_waiting(1)
-            quantise_projected(n)
+            finish(n)
+            if n + 1 < n_halves:
+                regroup(n + 1)
             if n + 2 < n_halves:
                 project(n + 2)
-            for unit in unlocked(n):
-                if unit[2] < FIRST_PAIRED:
-                    waiting.append(unit)
-                elif unit[2] == N_CHUNKS - 1:
-                    late.append((unit[0], unit[1]))
-            score_waiting(min(PER_SLOT, max(len(waiting) - n_scored[0] - HELD_BACK, 0)))
+            score_some()
 
         for n, pair in enumerate(sorted(late, key=lambda pair: (QUERY if pair[0] == KEY else KEY, pair[1]))):
             if n % DIRECT_EVERY == DIRECT_EVERY - 1:

@@ -217,12 +217,19 @@ def tile_contraattention_kernel(
                         bias=bias_cols[:, SLICES * s + j : SLICES * s + j + 1],
                     )
             in_flight[("by_slice", n)] = by_slice
+            if negated(n):
+                opposite = stage.tile([P, HALF * PACK], BF16, name="opposite", align_bytes=64)
+                nc.scalar.mul(
+                    out=opposite[:].rearrange("p (g i j) -> p g j i", i=4, j=SLICES),
+                    in_=by_slice[:].rearrange("p j (g i) -> p g j i", i=4),
+                    mul=-1.0,
+                )
+                in_flight[("opposite", n)] = opposite
 
         def regroup(n):
             s, c, e = halves[n]
             by_slice = in_flight[("by_slice", n)]
-            width = HALF * PACK * (2 if negated(n) else 1)
-            regrouped = single.tile([P, width], BF16, name="regrouped", align_bytes=64)
+            regrouped = single.tile([P, HALF * PACK], BF16, name="regrouped", align_bytes=64)
             regrouped_view = regrouped[:, 0 : HALF * PACK].rearrange("p (g i j) -> p g j i", i=4, j=SLICES)
             by_slice_view = by_slice[:].rearrange("p j (g i) -> p g j i", i=4)
             if c == 0:
@@ -240,24 +247,21 @@ def tile_contraattention_kernel(
                 nc.scalar.copy(out=regrouped_view, in_=by_slice_view)
             in_flight[("regrouped", n)] = regrouped
 
-        def negate(n):
-            regrouped = in_flight[("regrouped", n)]
-            nc.vector.tensor_scalar(
-                out=regrouped[:, HALF * PACK : 2 * HALF * PACK],
-                in0=regrouped[:, 0 : HALF * PACK],
-                scalar1=-1.0,
-                scalar2=None,
-                op0=ALU.mult,
-            )
-
         def quantise_projected(n):
             s, c, e = halves[n]
-            cols = slice(e * HALF, (e + (2 if negated(n) else 1)) * HALF)
+            cols = slice(e * HALF, (e + 1) * HALF)
             nc.vector.quantize_mx(
                 out=codes[s][c][:, cols].bitcast(FP8X4),
                 scales=planes[s][c][:, cols],
                 in_=in_flight[("regrouped", n)][:],
             )
+            if negated(n):
+                cols = slice(CHUNK, CHUNK + HALF)
+                nc.vector.quantize_mx(
+                    out=codes[s][c][:, cols].bitcast(FP8X4),
+                    scales=planes[s][c][:, cols],
+                    in_=in_flight[("opposite", n)][:],
+                )
 
         def unlocked(n):
             s, c, e = halves[n]
@@ -426,12 +430,8 @@ def tile_contraattention_kernel(
         for n in range(n_halves):
             if n + 4 < n_halves:
                 turn(n + 4)
-            if negated(n):
-                negate(n)
             if n + 3 < n_halves:
                 quantise_states(n + 3)
-            elif negated(n):
-                score_waiting(1)
             finish(n)
             if n + 1 < n_halves:
                 regroup(n + 1)

@@ -249,12 +249,6 @@ def tile_contraattention_kernel(
 
         def quantise_projected(n):
             s, c, e = halves[n]
-            cols = slice(e * HALF, (e + 1) * HALF)
-            nc.vector.quantize_mx(
-                out=codes[s][c][:, cols].bitcast(FP8X4),
-                scales=planes[s][c][:, cols],
-                in_=in_flight[("regrouped", n)][:],
-            )
             if negated(n):
                 cols = slice(CHUNK, CHUNK + HALF)
                 nc.vector.quantize_mx(
@@ -262,6 +256,12 @@ def tile_contraattention_kernel(
                     scales=planes[s][c][:, cols],
                     in_=in_flight[("opposite", n)][:],
                 )
+            cols = slice(e * HALF, (e + 1) * HALF)
+            nc.vector.quantize_mx(
+                out=codes[s][c][:, cols].bitcast(FP8X4),
+                scales=planes[s][c][:, cols],
+                in_=in_flight[("regrouped", n)][:],
+            )
 
         def unlocked(n):
             s, c, e = halves[n]

@@ -42,6 +42,9 @@ VECTOR_TURNS = ()
 REGROUP_CYCLE = 1
 GPSIMD_SHARE = 1
 REGROUP_BUFS = 1
+EARLY_SLOTS = 2
+STEPS_PER_SLOT = 2
+UNIT_BUFS = 7
 LAG = 3
 SUM_LAG = 2
 
@@ -74,7 +77,7 @@ def tile_contraattention_kernel(
         keep = ctx.enter_context(tc.tile_pool(name="keep", bufs=1))
         stage = ctx.enter_context(tc.tile_pool(name="stage", bufs=4))
         single = ctx.enter_context(tc.tile_pool(name="single", bufs=REGROUP_BUFS))
-        halving = ctx.enter_context(tc.tile_pool(name="halving", bufs=LAG + 2))
+        halving = ctx.enter_context(tc.tile_pool(name="halving", bufs=UNIT_BUFS))
         psum_t = ctx.enter_context(tc.psum_pool(name="psum_t", bufs=2))
         psum_proj = ctx.enter_context(tc.psum_pool(name="psum_proj", bufs=2))
         psum_logits = ctx.enter_context(tc.psum_pool(name="psum_logits", bufs=LOGIT_BANKS))
@@ -304,6 +307,8 @@ def tile_contraattention_kernel(
 
         units = []
         begun = []
+        summed = []
+        gate = [False]
 
         def unit_begin(s, t):
             difference = psum_t.tile([P, 2, HALF], F32, name="difference", tag="turned")
@@ -322,7 +327,12 @@ def tile_contraattention_kernel(
 
         def unit_middle(k):
             s, t, larger, odd_sb = units[k]
-            nc.gpsimd.tensor_tensor(out=larger[:], in0=larger[:], in1=odd_sb[:], op=ALU.add)
+            total = larger
+            if k == 0:
+                total = single.tile([P, CHUNK], F32, name="first_total", tag="regrouped", align_bytes=64)
+                units[k] = (s, t, total, odd_sb)
+            nc.gpsimd.tensor_tensor(out=total[:], in0=larger[:], in1=odd_sb[:], op=ALU.add)
+            summed.append(clock[0])
 
         def unit_end(k):
             s, t, larger, odd_sb = units[k]
@@ -368,10 +378,10 @@ def tile_contraattention_kernel(
             before = n_scored[0]
             score_waiting(due)
             n_scored[1] += n_scored[0] - before
-            for k in range(len(units)):
-                if begun[k] + 1 == clock[0]:
-                    unit_middle(k)
-                if begun[k] + LAG == clock[0]:
+            if gate[0] and len(summed) < len(units) and begun[len(summed)] < clock[0]:
+                unit_middle(len(summed))
+            for k in range(len(summed)):
+                if summed[k] + LAG - 1 == clock[0]:
                     unit_end(k)
             for t in range(N_TILES):
                 if t not in added and all(
@@ -389,6 +399,16 @@ def tile_contraattention_kernel(
                     waiting.append(unit)
                 elif unit[2] == N_CHUNKS - 1:
                     late.append((unit[0], unit[1]))
+
+        n_released = [0]
+
+        def release():
+            for pair in late[n_released[0] :]:
+                n_released[0] += 1
+                if n_released[0] % DIRECT_EVERY == 0:
+                    waiting.extend([(pair[0], pair[1], c) for c in range(FIRST_PAIRED, N_CHUNKS)])
+                else:
+                    paired.append(pair)
 
         def score_some():
             score_waiting(min(PER_SLOT, max(len(waiting) - n_scored[0] - HELD_BACK, 0)))
@@ -437,13 +457,15 @@ def tile_contraattention_kernel(
                 regroup(n + 1)
             if n + 2 < n_halves:
                 project(n + 2)
-            score_some()
+            if n < n_halves - EARLY_SLOTS:
+                score_some()
+            elif n + 1 < n_halves:
+                release()
+                for k in range(STEPS_PER_SLOT):
+                    step()
 
-        for n, pair in enumerate(sorted(late, key=lambda pair: (QUERY if pair[0] == KEY else KEY, pair[1]))):
-            if n % DIRECT_EVERY == DIRECT_EVERY - 1:
-                waiting.extend([(pair[0], pair[1], c) for c in range(FIRST_PAIRED, N_CHUNKS)])
-            else:
-                paired.append(pair)
+        gate[0] = True
+        release()
         while len(added) < N_TILES:
             step()
         sums = sums_of[0]

@@ -37,7 +37,7 @@ PER_SLOT = 3
 HELD_BACK = 1
 FIRST_PAIRED = 2
 DIRECT_EVERY = 5
-ALONE_PER_STEPS = (4, 3)
+ALONE_PER_STEPS = (5, 3)
 VECTOR_TURNS = ()
 REGROUP_CYCLE = 1
 GPSIMD_SHARE = 1

@@ -39,9 +39,9 @@ FIRST_PAIRED = 2
 DIRECT_EVERY = 5
 ALONE_PER_STEPS = (5, 3)
 VECTOR_TURNS = ()
-REGROUP_CYCLE = 1
-GPSIMD_SHARE = 1
+VECTOR_BIAS = (0, 1, 2)
 REGROUP_BUFS = 1
+FACTORS_SLOT = 8
 EARLY_SLOTS = 2
 STEPS_PER_SLOT = 2
 UNIT_BUFS = 7
@@ -104,18 +104,19 @@ def tile_contraattention_kernel(
         make_identity(nc, ident_f32[:])
         make_identity(nc, ident_bf16[:])
 
-        def load_states(s, c):
+        def load_half(s, c, e):
             rows = states[s][c * CHUNK : (c + 1) * CHUNK, :].rearrange("(i p e) d -> e p i d", p=P, e=2)
-            for e in range(2):
-                nc.sync.dma_start(
-                    out=raw[s][c][:, e * TILES_PER_HALF : (e + 1) * TILES_PER_HALF, :],
-                    in_=rows[e],
-                )
+            nc.sync.dma_start(
+                out=raw[s][c][:, e * TILES_PER_HALF : (e + 1) * TILES_PER_HALF, :],
+                in_=rows[e],
+            )
 
-        def load_weight(s):
+        def load_planes(s):
             rows = weight_scales[s].rearrange("g (b r) n -> (g r) b n", r=PACK)
             for r in range(PACK):
                 nc.sync.dma_start(out=w_planes[s][r:P:32, :].bitcast(I32), in_=rows[r].bitcast(I32))
+
+        def load_codes(s):
             nc.sync.dma_start(
                 out=w_codes[s][:].bitcast(I32),
                 in_=weight_words[s].rearrange("g p n t -> (g p) (n t)").bitcast(I32),
@@ -129,20 +130,28 @@ def tile_contraattention_kernel(
         nc.vector.memset(mask_sb[:], 1.0)
         scale_sb = keep.tile([P, 1], BF16, name="scale_sb")
 
-        nc.sync.dma_start(out=scale_sb[:], in_=logit_scale.partition_broadcast(P))
-        load_states(KEY, 0)
-        load_weight(KEY)
-        for s in (KEY, QUERY):
+        def load_bias(s):
             nc.sync.dma_start(
                 out=bias_rows[SLICES * s : SLICES * (s + 1), :],
                 in_=biases[s].rearrange("(j p) -> j p", p=P),
             )
-        load_states(QUERY, 0)
-        load_weight(QUERY)
-        nc.sync.dma_start(out=mask_sb[0:N_SEQ, :], in_=attention_mask)
+
+        load_half(KEY, 0, 0)
+        load_planes(KEY)
+        load_codes(KEY)
+        load_half(KEY, 0, 1)
+        load_bias(KEY)
+        load_bias(QUERY)
+        load_half(QUERY, 0, 0)
+        load_codes(QUERY)
+        load_planes(QUERY)
+        load_half(QUERY, 0, 1)
         for c in range(1, N_CHUNKS):
-            load_states(KEY, c)
-            load_states(QUERY, c)
+            for s in (KEY, QUERY):
+                for e in range(2):
+                    load_half(s, c, e)
+        nc.sync.dma_start(out=mask_sb[0:N_SEQ, :], in_=attention_mask)
+        nc.sync.dma_start(out=scale_sb[:], in_=logit_scale.partition_broadcast(P))
 
         last_window = N_SEQ - SEQ_PER_TILE
         selector = keep.tile([P, last_window + P], F32, name="selector")
@@ -155,7 +164,9 @@ def tile_contraattention_kernel(
         scaled = keep.tile([P, N_SEQ + P], F32, name="scaled")
         nc.vector.memset(scaled[:], 0.0)
         exp_scale = keep.tile([P, 1], F32, name="exp_scale")
-        nc.scalar.activation(out=exp_scale[:], in_=scale_sb[:], func=ACT.Exp)
+        table_probe = keep.tile([P, 1], F32, name="table_probe")
+        nc.vector.memset(table_probe[:], 0.0)
+        nc.scalar.activation(out=exp_scale[:], in_=table_probe[:], func=ACT.Exp)
         bias_cols = keep.tile([P, 2 * SLICES], F32, name="bias_cols")
 
         halves = [(s, c, e) for c in range(N_CHUNKS) for s in (KEY, QUERY) for e in range(2)]
@@ -197,6 +208,24 @@ def tile_contraattention_kernel(
         def project(n):
             s, c, e = halves[n]
             x_codes, x_planes = in_flight[("x", n)]
+            if n in VECTOR_BIAS:
+                accs = []
+                for i in range(TILES_PER_HALF):
+                    rows = slice(i * P, (i + 1) * P)
+                    acc = psum_logits.tile([P, SLICES, P], F32, name="acc_v", tag="logits")
+                    for j in range(SLICES):
+                        nc.tensor.matmul_mx(
+                            out=acc[:, j, :],
+                            lhsT=w_codes[s][:, j * P : (j + 1) * P].bitcast(FP8X4),
+                            lhsT_scale=w_planes[s][:, j * P : (j + 1) * P],
+                            rhs=x_codes[:, rows].bitcast(FP8X4),
+                            rhs_scale=x_planes[:, rows],
+                            start=True,
+                            stop=True,
+                        )
+                    accs.append(acc)
+                in_flight[("accs", n)] = accs
+                return
             by_slice = stage.tile([P, SLICES, HALF], BF16, name="by_slice")
             for pair in range(SLICES // 2):
                 acc = psum_proj.tile([P, 2, HALF], F32, name="acc", tag="acc")
@@ -231,23 +260,27 @@ def tile_contraattention_kernel(
 
         def regroup(n):
             s, c, e = halves[n]
+            if n in VECTOR_BIAS:
+                regrouped = stage.tile([P, HALF * PACK], BF16, name="regrouped_v", align_bytes=64)
+                for i in range(TILES_PER_HALF):
+                    nc.vector.tensor_tensor(
+                        out=regrouped[:, i * P * PACK : (i + 1) * P * PACK].rearrange("p (r j) -> p r j", j=SLICES),
+                        in0=in_flight[("accs", n)][i][:].rearrange("p j r -> p r j"),
+                        in1=bias_cols[:, SLICES * s : SLICES * (s + 1)].unsqueeze(1).to_broadcast([P, P, SLICES]),
+                        op=ALU.add,
+                    )
+                in_flight[("regrouped", n)] = regrouped
+                return
             by_slice = in_flight[("by_slice", n)]
             regrouped = single.tile([P, HALF * PACK], BF16, name="regrouped", align_bytes=64)
-            regrouped_view = regrouped[:, 0 : HALF * PACK].rearrange("p (g i j) -> p g j i", i=4, j=SLICES)
-            by_slice_view = by_slice[:].rearrange("p j (g i) -> p g j i", i=4)
-            if c == 0:
-                nc.vector.tensor_copy(out=regrouped_view, in_=by_slice_view)
-            elif n % REGROUP_CYCLE < GPSIMD_SHARE:
-                nc.gpsimd.tensor_scalar(
-                    out=regrouped[:, 0 : HALF * PACK].rearrange("p (r j) -> p r j", j=SLICES),
-                    in0=by_slice[:].rearrange("p j r -> p r j"),
-                    scalar1=1.0,
-                    scalar2=0.0,
-                    op0=ALU.mult,
-                    op1=ALU.add,
-                )
-            else:
-                nc.scalar.copy(out=regrouped_view, in_=by_slice_view)
+            nc.gpsimd.tensor_scalar(
+                out=regrouped[:].rearrange("p (r j) -> p r j", j=SLICES),
+                in0=by_slice[:].rearrange("p j r -> p r j"),
+                scalar1=1.0,
+                scalar2=0.0,
+                op0=ALU.mult,
+                op1=ALU.add,
+            )
             in_flight[("regrouped", n)] = regrouped
 
         def quantise_projected(n):
@@ -390,6 +423,28 @@ def tile_contraattention_kernel(
                 ):
                     add_up(t)
 
+        mask_sum = keep.tile([P, 1], F32, name="mask_sum")
+        inv_mask_sum = keep.tile([P, 1], F32, name="inv_mask_sum")
+        factors = keep.tile([P, 2, N_SEQ], F32, name="factors")
+
+        def make_factors():
+            nc.vector.reciprocal(out=inv_mask_sum[:], in_=mask_sum[:])
+            nc.vector.tensor_scalar(
+                out=factors[:, QUERY, :],
+                in0=exp_scale[:].to_broadcast([P, N_SEQ]),
+                scalar1=inv_mask_sum[:, 0:1],
+                scalar2=0.5,
+                op0=ALU.mult,
+                op1=ALU.mult,
+            )
+            nc.vector.tensor_scalar(
+                out=factors[:, KEY, :],
+                in0=exp_scale[:].to_broadcast([P, N_SEQ]),
+                scalar1=0.5 / SEQ,
+                scalar2=None,
+                op0=ALU.mult,
+            )
+
         late = []
 
         def finish(n):
@@ -416,38 +471,40 @@ def tile_contraattention_kernel(
         turn(0)
         turn(1)
         quantise_states(0)
-        turn(2)
-        quantise_states(1)
         bias_t = psum_t.tile([P, P], BF16, name="bias_t", tag="turned")
         nc.tensor.transpose(bias_t[:], bias_rows[:], ident_bf16[:])
         nc.vector.tensor_copy(out=bias_cols[:], in_=bias_t[:, 0 : 2 * SLICES])
         project(0)
-        turn(3)
-        quantise_states(2)
-        regroup(0)
+        turn(2)
+        quantise_states(1)
         project(1)
-        mask_sum = keep.tile([P, 1], F32, name="mask_sum")
-        nc.vector.tensor_reduce(out=mask_sum[:], in_=mask_sb[:], axis=AXIS_X, op=ALU.add)
-        inv_mask_sum = keep.tile([P, 1], F32, name="inv_mask_sum")
-        nc.vector.reciprocal(out=inv_mask_sum[:], in_=mask_sum[:])
-        factors = keep.tile([P, 2, N_SEQ], F32, name="factors")
-        nc.vector.tensor_scalar(
-            out=factors[:, QUERY, :],
-            in0=exp_scale[:].to_broadcast([P, N_SEQ]),
-            scalar1=inv_mask_sum[:, 0:1],
-            scalar2=0.5,
-            op0=ALU.mult,
-            op1=ALU.mult,
-        )
-        nc.vector.tensor_scalar(
-            out=factors[:, KEY, :],
-            in0=exp_scale[:].to_broadcast([P, N_SEQ]),
-            scalar1=0.5 / SEQ,
-            scalar2=None,
-            op0=ALU.mult,
-        )
+        regroup(0)
+        quantise_states(2)
+        turn(3)
+        finish(0)
+        project(2)
+        regroup(1)
+        quantise_states(3)
+        turn(4)
+        regroup(2)
+        project(3)
+        finish(1)
+        finish(2)
+        quantise_states(4)
+        score_some()
+        regroup(3)
+        turn(5)
+        project(4)
+        turn(6)
+        finish(3)
+        regroup(4)
+        quantise_states(5)
+        score_some()
+        project(5)
+        turn(7)
+        quantise_states(6)
 
-        for n in range(n_halves):
+        for n in range(4, n_halves):
             if n + 4 < n_halves:
                 turn(n + 4)
             if n + 3 < n_halves:
@@ -457,6 +514,11 @@ def tile_contraattention_kernel(
                 regroup(n + 1)
             if n + 2 < n_halves:
                 project(n + 2)
+            if n == FACTORS_SLOT - 1:
+                nc.scalar.activation(out=exp_scale[:], in_=scale_sb[:], func=ACT.Exp)
+                nc.vector.tensor_reduce(out=mask_sum[:], in_=mask_sb[:], axis=AXIS_X, op=ALU.add)
+            if n == FACTORS_SLOT:
+                make_factors()
             if n < n_halves - EARLY_SLOTS:
                 score_some()
             elif n + 1 < n_halves:

@@ -122,6 +122,8 @@ def tile_contraattention_kernel(
                 in_=weight_words[s].rearrange("g p n t -> (g p) (n t)").bitcast(I32),
             )
 
+        zeros = keep.tile([P, CHUNK], BF16, name="zeros")
+        nc.vector.memset(zeros[:], 0.0)
         for s in (KEY, QUERY):
             nc.vector.memset(w_planes[s][:].bitcast(I32), 0)
         bias_rows = keep.tile([P, P], BF16, name="bias_rows")
@@ -423,6 +425,11 @@ def tile_contraattention_kernel(
                 ):
                     add_up(t)
 
+        def warm_up(n_matmuls):
+            for k in range(n_matmuls):
+                idle = psum_proj.tile([P, CHUNK], F32, name="idle", tag="acc")
+                nc.tensor.matmul(out=idle[:], lhsT=zeros[:, 0:P], rhs=zeros[:], start=True, stop=True)
+
         mask_sum = keep.tile([P, 1], F32, name="mask_sum")
         inv_mask_sum = keep.tile([P, 1], F32, name="inv_mask_sum")
         factors = keep.tile([P, 2, N_SEQ], F32, name="factors")
@@ -468,7 +475,9 @@ def tile_contraattention_kernel(
         def score_some():
             score_waiting(min(PER_SLOT, max(len(waiting) - n_scored[0] - HELD_BACK, 0)))
 
+        warm_up(4)
         turn(0)
+        warm_up(2)
         turn(1)
         quantise_states(0)
         bias_t = psum_t.tile([P, P], BF16, name="bias_t", tag="turned")

@@ -41,6 +41,7 @@ ALONE_PER_STEPS = (5, 3)
 VECTOR_TURNS = ()
 VECTOR_BIAS = (0, 1, 2)
 REGROUP_BUFS = 1
+PAIRED_TURNS = 6
 FACTORS_SLOT = 8
 EARLY_SLOTS = 2
 STEPS_PER_SLOT = 2
@@ -514,8 +515,11 @@ def tile_contraattention_kernel(
         quantise_states(6)
 
         for n in range(4, n_halves):
-            if n + 4 < n_halves:
+            if n + 4 < n_halves and n < PAIRED_TURNS:
                 turn(n + 4)
+            elif n + 4 < n_halves and n % 2 == 0:
+                turn(n + 4)
+                turn(n + 5)
             if n + 3 < n_halves:
                 quantise_states(n + 3)
             finish(n)

@@ -42,7 +42,6 @@ VECTOR_TURNS = ()
 VECTOR_BIAS = (0, 1, 2)
 REGROUP_BUFS = 1
 PAIRED_TURNS = 6
-FACTORS_SLOT = 8
 EARLY_SLOTS = 2
 STEPS_PER_SLOT = 2
 UNIT_BUFS = 7
@@ -84,7 +83,7 @@ def tile_contraattention_kernel(
         psum_logits = ctx.enter_context(tc.psum_pool(name="psum_logits", bufs=LOGIT_BANKS))
 
         raw = [
-            [keep.tile([P, TILES_PER_CHUNK, FEATURES], BF16, name="raw_%d_%d" % (s, c)) for c in range(N_CHUNKS)]
+            [keep.tile([P, TILES_PER_HALF, 2, FEATURES], BF16, name="raw_%d_%d" % (s, c)) for c in range(N_CHUNKS)]
             for s in (QUERY, KEY)
         ]
         w_codes = [keep.tile([P, FEATURES], U32, name="w_codes_%d" % s, align_bytes=64) for s in (QUERY, KEY)]
@@ -105,11 +104,15 @@ def tile_contraattention_kernel(
         make_identity(nc, ident_f32[:])
         make_identity(nc, ident_bf16[:])
 
-        def load_half(s, c, e):
-            rows = states[s][c * CHUNK : (c + 1) * CHUNK, :].rearrange("(i p e) d -> e p i d", p=P, e=2)
+        def load_group(s, c, i):
+            tokens = states[s][c * CHUNK + i * HALF : c * CHUNK + (i + 1) * HALF, :]
             nc.sync.dma_start(
-                out=raw[s][c][:, e * TILES_PER_HALF : (e + 1) * TILES_PER_HALF, :],
-                in_=rows[e],
+                out=raw[s][c][:, i : i + 1, :, :], in_=tokens.rearrange("(i p e) d -> p i e d", i=1, e=2)
+            )
+
+        def load_chunk(s, c):
+            nc.sync.dma_start(
+                out=raw[s][c][:], in_=states[s][c * CHUNK : (c + 1) * CHUNK, :].rearrange("(i p e) d -> p i e d", p=P, e=2)
             )
 
         def load_planes(s):
@@ -124,9 +127,9 @@ def tile_contraattention_kernel(
             )
 
         zeros = keep.tile([P, CHUNK], BF16, name="zeros")
+        nc.vector.memset(w_planes[KEY][:].bitcast(I32), 0)
         nc.vector.memset(zeros[:], 0.0)
-        for s in (KEY, QUERY):
-            nc.vector.memset(w_planes[s][:].bitcast(I32), 0)
+        nc.vector.memset(w_planes[QUERY][:].bitcast(I32), 0)
         bias_rows = keep.tile([P, P], BF16, name="bias_rows")
         nc.vector.memset(bias_rows[:], 0.0)
         mask_sb = keep.tile([P, SEQ], BF16, name="mask_sb")
@@ -139,22 +142,21 @@ def tile_contraattention_kernel(
                 in_=biases[s].rearrange("(j p) -> j p", p=P),
             )
 
-        load_half(KEY, 0, 0)
+        load_group(KEY, 0, 0)
         load_planes(KEY)
         load_codes(KEY)
-        load_half(KEY, 0, 1)
+        load_group(KEY, 0, 1)
         load_bias(KEY)
         load_bias(QUERY)
-        load_half(QUERY, 0, 0)
+        load_group(QUERY, 0, 0)
         load_codes(QUERY)
         load_planes(QUERY)
-        load_half(QUERY, 0, 1)
-        for c in range(1, N_CHUNKS):
-            for s in (KEY, QUERY):
-                for e in range(2):
-                    load_half(s, c, e)
+        load_group(QUERY, 0, 1)
         nc.sync.dma_start(out=mask_sb[0:N_SEQ, :], in_=attention_mask)
         nc.sync.dma_start(out=scale_sb[:], in_=logit_scale.partition_broadcast(P))
+        for c in range(1, N_CHUNKS):
+            for s in (KEY, QUERY):
+                load_chunk(s, c)
 
         last_window = N_SEQ - SEQ_PER_TILE
         selector = keep.tile([P, last_window + P], F32, name="selector")
@@ -188,7 +190,7 @@ def tile_contraattention_kernel(
                 for u in range(2):
                     nc.tensor.transpose(
                         turned[:, i, u, :],
-                        raw_words[:, e * TILES_PER_HALF + i, u : FEATURES // 2 : 2],
+                        raw_words[:, e, i, u : FEATURES // 2 : 2] if c == 0 else raw_words[:, i, e, u : FEATURES // 2 : 2],
                         ident_f32[:],
                     )
             grouped = stage.tile([P, HALF * PACK], BF16, name="grouped", align_bytes=64)
@@ -295,6 +297,15 @@ def tile_contraattention_kernel(
                     scales=planes[s][c][:, cols],
                     in_=in_flight[("opposite", n)][:],
                 )
+            if c == 0:
+                for i in range(2):
+                    cols = slice((2 * i + e) * P, (2 * i + e + 1) * P)
+                    nc.vector.quantize_mx(
+                        out=codes[s][c][:, cols].bitcast(FP8X4),
+                        scales=planes[s][c][:, cols],
+                        in_=in_flight[("regrouped", n)][:, i * P * PACK : (i + 1) * P * PACK],
+                    )
+                return
             cols = slice(e * HALF, (e + 1) * HALF)
             nc.vector.quantize_mx(
                 out=codes[s][c][:, cols].bitcast(FP8X4),
@@ -305,8 +316,9 @@ def tile_contraattention_kernel(
         def unlocked(n):
             s, c, e = halves[n]
             other_chunks = c if s == KEY else c + 1
-            first = c * TILES_PER_CHUNK + e * TILES_PER_HALF
-            new = [(s, t, o) for t in range(first, first + TILES_PER_HALF) for o in range(other_chunks)]
+            first = c * TILES_PER_CHUNK
+            tiles = (first + e, first + e + 2) if c == 0 else (first + 2 * e, first + 2 * e + 1)
+            new = [(s, t, o) for t in tiles for o in range(other_chunks)]
             if e == 1:
                 new.extend([(1 - s, t, c) for t in range(other_chunks * TILES_PER_CHUNK)])
             return new
@@ -408,11 +420,12 @@ def tile_contraattention_kernel(
 
         def step():
             clock[0] += 1
-            if len(units) < len(paired):
-                unit_begin(*paired[len(units)])
             due = (clock[0] * ALONE_PER_STEPS[0]) // ALONE_PER_STEPS[1] - n_scored[1]
             before = n_scored[0]
-            score_waiting(due)
+            score_waiting(1)
+            if len(units) < len(paired):
+                unit_begin(*paired[len(units)])
+            score_waiting(due - 1)
             n_scored[1] += n_scored[0] - before
             if gate[0] and len(summed) < len(units) and begun[len(summed)] < clock[0]:
                 unit_middle(len(summed))
@@ -436,6 +449,7 @@ def tile_contraattention_kernel(
         factors = keep.tile([P, 2, N_SEQ], F32, name="factors")
 
         def make_factors():
+            nc.vector.tensor_reduce(out=mask_sum[:], in_=mask_sb[:], axis=AXIS_X, op=ALU.add)
             nc.vector.reciprocal(out=inv_mask_sum[:], in_=mask_sum[:])
             nc.vector.tensor_scalar(
                 out=factors[:, QUERY, :],
@@ -496,6 +510,7 @@ def tile_contraattention_kernel(
         regroup(1)
         quantise_states(3)
         turn(4)
+        nc.scalar.activation(out=exp_scale[:], in_=scale_sb[:], func=ACT.Exp)
         regroup(2)
         project(3)
         finish(1)
@@ -505,6 +520,7 @@ def tile_contraattention_kernel(
         regroup(3)
         turn(5)
         project(4)
+        make_factors()
         turn(6)
         finish(3)
         regroup(4)
@@ -527,11 +543,6 @@ def tile_contraattention_kernel(
                 regroup(n + 1)
             if n + 2 < n_halves:
                 project(n + 2)
-            if n == FACTORS_SLOT - 1:
-                nc.scalar.activation(out=exp_scale[:], in_=scale_sb[:], func=ACT.Exp)
-                nc.vector.tensor_reduce(out=mask_sum[:], in_=mask_sb[:], axis=AXIS_X, op=ALU.add)
-            if n == FACTORS_SLOT:
-                make_factors()
             if n < n_halves - EARLY_SLOTS:
                 score_some()
             elif n + 1 < n_halves:

@@ -88,15 +88,23 @@ def tile_contraattention_kernel(
         ]
         w_codes = [keep.tile([P, FEATURES], U32, name="w_codes_%d" % s, align_bytes=64) for s in (QUERY, KEY)]
         w_planes = [keep.tile([P, FEATURES], U8, name="w_planes_%d" % s, align_bytes=64) for s in (QUERY, KEY)]
-        widths = [CHUNK + (HALF if c >= FIRST_PAIRED else 0) for c in range(N_CHUNKS)]
         codes = [
-            [keep.tile([P, widths[c]], U32, name="codes_%d_%d" % (s, c), align_bytes=64) for c in range(N_CHUNKS)]
+            [keep.tile([P, CHUNK], U32, name="codes_%d_%d" % (s, c), align_bytes=64) for c in range(FIRST_PAIRED)]
             for s in (QUERY, KEY)
         ]
         planes = [
-            [keep.tile([P, widths[c]], U8, name="planes_%d_%d" % (s, c), align_bytes=64) for c in range(N_CHUNKS)]
+            [keep.tile([P, CHUNK], U8, name="planes_%d_%d" % (s, c), align_bytes=64) for c in range(FIRST_PAIRED)]
             for s in (QUERY, KEY)
         ]
+        pair_codes = [keep.tile([P, 3 * CHUNK], U32, name="pair_codes_%d" % s, align_bytes=64) for s in (QUERY, KEY)]
+        pair_planes = [keep.tile([P, 3 * CHUNK], U8, name="pair_planes_%d" % s, align_bytes=64) for s in (QUERY, KEY)]
+
+        def quantised(s, c, block, first, width):
+            if c < FIRST_PAIRED:
+                cols = slice(block * HALF + first, block * HALF + first + width)
+                return codes[s][c][:, cols], planes[s][c][:, cols]
+            start = block * CHUNK + (c - FIRST_PAIRED) * HALF + first
+            return pair_codes[s][:, start : start + width], pair_planes[s][:, start : start + width]
         maxima = [keep.tile([P, 2, N_SEQ], F32, name="maxima_%d" % t) for t in range(N_TILES)]
 
         ident_f32 = keep.tile([P, P], F32, name="ident_f32")
@@ -291,26 +299,22 @@ def tile_contraattention_kernel(
         def quantise_projected(n):
             s, c, e = halves[n]
             if negated(n):
-                cols = slice(CHUNK, CHUNK + HALF)
+                out_codes, out_planes = quantised(s, c, 2, 0, HALF)
                 nc.vector.quantize_mx(
-                    out=codes[s][c][:, cols].bitcast(FP8X4),
-                    scales=planes[s][c][:, cols],
-                    in_=in_flight[("opposite", n)][:],
+                    out=out_codes.bitcast(FP8X4), scales=out_planes, in_=in_flight[("opposite", n)][:]
                 )
             if c == 0:
                 for i in range(2):
-                    cols = slice((2 * i + e) * P, (2 * i + e + 1) * P)
+                    out_codes, out_planes = quantised(s, c, i, e * P, P)
                     nc.vector.quantize_mx(
-                        out=codes[s][c][:, cols].bitcast(FP8X4),
-                        scales=planes[s][c][:, cols],
+                        out=out_codes.bitcast(FP8X4),
+                        scales=out_planes,
                         in_=in_flight[("regrouped", n)][:, i * P * PACK : (i + 1) * P * PACK],
                     )
                 return
-            cols = slice(e * HALF, (e + 1) * HALF)
+            out_codes, out_planes = quantised(s, c, e, 0, HALF)
             nc.vector.quantize_mx(
-                out=codes[s][c][:, cols].bitcast(FP8X4),
-                scales=planes[s][c][:, cols],
-                in_=in_flight[("regrouped", n)][:],
+                out=out_codes.bitcast(FP8X4), scales=out_planes, in_=in_flight[("regrouped", n)][:]
             )
 
         def unlocked(n):
@@ -323,15 +327,16 @@ def tile_contraattention_kernel(
                 new.extend([(1 - s, t, c) for t in range(other_chunks * TILES_PER_CHUNK)])
             return new
 
-        def product(out, s, t, c, first, width, start, stop):
-            o = 1 - s
-            cols = slice((t % TILES_PER_CHUNK) * P, (t % TILES_PER_CHUNK + 1) * P)
+        def product(out, s, t, c, block, width, start, stop):
+            chunk, place = divmod(t, TILES_PER_CHUNK)
+            lhs_codes, lhs_planes = quantised(s, chunk, place // TILES_PER_HALF, place % TILES_PER_HALF * P, P)
+            rhs_codes, rhs_planes = quantised(1 - s, c, block, 0, width)
             nc.tensor.matmul_mx(
                 out=out,
-                lhsT=codes[s][t // TILES_PER_CHUNK][:, cols].bitcast(FP8X4),
-                lhsT_scale=planes[s][t // TILES_PER_CHUNK][:, cols],
-                rhs=codes[o][c][:, first : first + width].bitcast(FP8X4),
-                rhs_scale=planes[o][c][:, first : first + width],
+                lhsT=lhs_codes.bitcast(FP8X4),
+                lhsT_scale=lhs_planes,
+                rhs=rhs_codes.bitcast(FP8X4),
+                rhs_scale=rhs_planes,
                 start=start,
                 stop=stop,
             )
@@ -344,7 +349,11 @@ def tile_contraattention_kernel(
 
         def score(s, t, c):
             logits = psum_logits.tile([P, CHUNK], F32, name="logits")
-            product(logits[:], s, t, c, 0, CHUNK, True, True)
+            if c < FIRST_PAIRED:
+                product(logits[:], s, t, c, 0, CHUNK, True, True)
+            else:
+                for e in range(2):
+                    product(logits[:, e * HALF : (e + 1) * HALF], s, t, c, e, HALF, True, True)
             nc.vector.tensor_reduce(
                 out=maxima[t][:, s, c * SEQ_PER_CHUNK : (c + 1) * SEQ_PER_CHUNK],
                 in_=logits[:].rearrange("p (e b m) -> p b e m", e=2, m=PAIRS),
@@ -359,17 +368,15 @@ def tile_contraattention_kernel(
         gate = [False]
 
         def unit_begin(s, t):
-            difference = psum_t.tile([P, 2, HALF], F32, name="difference", tag="turned")
-            odd = psum_proj.tile([P, 2, HALF], F32, name="odd", tag="acc")
-            for g in range(2):
-                product(difference[:, g, :], s, t, FIRST_PAIRED + g, 0, HALF, True, False)
-                product(difference[:, g, :], s, t, FIRST_PAIRED + g, CHUNK, HALF, False, True)
-            for g in range(2):
-                product(odd[:, g, :], s, t, FIRST_PAIRED + g, HALF, HALF, True, True)
+            difference = psum_t.tile([P, CHUNK], F32, name="difference", tag="turned")
+            odd = psum_proj.tile([P, CHUNK], F32, name="odd", tag="acc")
+            product(difference[:], s, t, FIRST_PAIRED, 0, CHUNK, True, False)
+            product(difference[:], s, t, FIRST_PAIRED, 2, CHUNK, False, True)
+            product(odd[:], s, t, FIRST_PAIRED, 1, CHUNK, True, True)
             larger = halving.tile([P, CHUNK], F32, name="larger")
-            nc.scalar.activation(out=larger[:], in_=difference[:].rearrange("p g n -> p (g n)"), func=ACT.Relu)
+            nc.scalar.activation(out=larger[:], in_=difference[:], func=ACT.Relu)
             odd_sb = halving.tile([P, CHUNK], F32, name="odd_sb")
-            nc.scalar.copy(out=odd_sb[:], in_=odd[:].rearrange("p g n -> p (g n)"))
+            nc.scalar.copy(out=odd_sb[:], in_=odd[:])
             units.append((s, t, larger, odd_sb))
             begun.append(clock[0])
 

from contextlib import ExitStack

import concourse.mybir as mybir
from concourse.masks import make_identity

F32 = mybir.dt.float32
BF16 = mybir.dt.bfloat16
I32 = mybir.dt.int32
U32 = mybir.dt.uint32
U8 = mybir.dt.uint8
FP8X4 = mybir.dt.float8_e4m3fn_x4
ALU = mybir.AluOpType
ACT = mybir.ActivationFunctionType
AXIS_X = mybir.AxisListType.X
AXIS_XY = mybir.AxisListType.XY

P = 128
PACK = 4
N_SEQ = 32
SEQ = 64
FEATURES = 512
TOKENS = N_SEQ * SEQ
CHUNK = 512
N_CHUNKS = TOKENS // CHUNK
TILES_PER_CHUNK = CHUNK // P
N_TILES = TOKENS // P
SEQ_PER_CHUNK = CHUNK // SEQ
SLICES = FEATURES // P
HALF = CHUNK // 2
TILES_PER_HALF = HALF // P
PAIRS = SEQ // 2
SEQ_PER_TILE = P // PAIRS
QUERY = 0
KEY = 1
LOGIT_BANKS = 4
PER_SLOT = 3
HELD_BACK = 1
FIRST_PAIRED = 2
DIRECT_EVERY = 5
ALONE_PER_STEPS = (5, 3)
VECTOR_TURNS = ()
VECTOR_BIAS = (0, 1, 2)
REGROUP_BUFS = 1
PAIRED_TURNS = 6
EARLY_SLOTS = 2
STEPS_PER_SLOT = 2
UNIT_BUFS = 7
LAG = 3
SUM_LAG = 2

FLOPS = 2 * 2 * TOKENS * FEATURES * FEATURES + 2 * TOKENS * TOKENS * FEATURES


def tile_contraattention_kernel(
    tc,
    query_states,
    key_states,
    attention_mask,
    Wq_words,
    Wq_scales,
    bq,
    Wk_words,
    Wk_scales,
    bk,
    logit_scale,
    out_0,
    out_1,
):
    nc = tc.nc
    states = (query_states.flatten_outer_dims(), key_states.flatten_outer_dims())
    weight_words = (Wq_words, Wk_words)
    weight_scales = (Wq_scales, Wk_scales)
    biases = (bq, bk)

    with ExitStack() as ctx:
        ctx.enter_context(tc.manual_schedule())
        keep = ctx.enter_context(tc.tile_pool(name="keep", bufs=1))
        stage = ctx.enter_context(tc.tile_pool(name="stage", bufs=4))
        single = ctx.enter_context(tc.tile_pool(name="single", bufs=REGROUP_BUFS))
        halving = ctx.enter_context(tc.tile_pool(name="halving", bufs=UNIT_BUFS))
        psum_t = ctx.enter_context(tc.psum_pool(name="psum_t", bufs=2))
        psum_proj = ctx.enter_context(tc.psum_pool(name="psum_proj", bufs=2))
        psum_logits = ctx.enter_context(tc.psum_pool(name="psum_logits", bufs=LOGIT_BANKS))

        raw = [
            [keep.tile([P, TILES_PER_HALF, 2, FEATURES], BF16, name="raw_%d_%d" % (s, c)) for c in range(N_CHUNKS)]
            for s in (QUERY, KEY)
        ]
        w_codes = [keep.tile([P, FEATURES], U32, name="w_codes_%d" % s, align_bytes=64) for s in (QUERY, KEY)]
        w_planes = [keep.tile([P, FEATURES], U8, name="w_planes_%d" % s, align_bytes=64) for s in (QUERY, KEY)]
        codes = [
            [keep.tile([P, CHUNK], U32, name="codes_%d_%d" % (s, c), align_bytes=64) for c in range(FIRST_PAIRED)]
            for s in (QUERY, KEY)
        ]
        planes = [
            [keep.tile([P, CHUNK], U8, name="planes_%d_%d" % (s, c), align_bytes=64) for c in range(FIRST_PAIRED)]
            for s in (QUERY, KEY)
        ]
        pair_codes = [keep.tile([P, 3 * CHUNK], U32, name="pair_codes_%d" % s, align_bytes=64) for s in (QUERY, KEY)]
        pair_planes = [keep.tile([P, 3 * CHUNK], U8, name="pair_planes_%d" % s, align_bytes=64) for s in (QUERY, KEY)]

        def quantised(s, c, block, first, width):
            if c < FIRST_PAIRED:
                cols = slice(block * HALF + first, block * HALF + first + width)
                return codes[s][c][:, cols], planes[s][c][:, cols]
            start = block * CHUNK + (c - FIRST_PAIRED) * HALF + first
            return pair_codes[s][:, start : start + width], pair_planes[s][:, start : start + width]
        maxima = [keep.tile([P, 2, N_SEQ], F32, name="maxima_%d" % t) for t in range(N_TILES)]

        ident_f32 = keep.tile([P, P], F32, name="ident_f32")
        ident_bf16 = keep.tile([P, P], BF16, name="ident_bf16")
        make_identity(nc, ident_f32[:])
        make_identity(nc, ident_bf16[:])

        def load_group(s, c, i):
            tokens = states[s][c * CHUNK + i * HALF : c * CHUNK + (i + 1) * HALF, :]
            nc.sync.dma_start(
                out=raw[s][c][:, i : i + 1, :, :], in_=tokens.rearrange("(i p e) d -> p i e d", i=1, e=2)
            )

        def load_chunk(s, c):
            nc.sync.dma_start(
                out=raw[s][c][:], in_=states[s][c * CHUNK : (c + 1) * CHUNK, :].rearrange("(i p e) d -> p i e d", p=P, e=2)
            )

        def load_planes(s):
            rows = weight_scales[s].rearrange("g (b r) n -> (g r) b n", r=PACK)
            for r in range(PACK):
                nc.sync.dma_start(out=w_planes[s][r:P:32, :].bitcast(I32), in_=rows[r].bitcast(I32))

        def load_codes(s):
            nc.sync.dma_start(
                out=w_codes[s][:].bitcast(I32),
                in_=weight_words[s].rearrange("g p n t -> (g p) (n t)").bitcast(I32),
            )

        zeros = keep.tile([P, CHUNK], BF16, name="zeros")
        nc.vector.memset(w_planes[KEY][:].bitcast(I32), 0)
        nc.vector.memset(zeros[:], 0.0)
        nc.vector.memset(w_planes[QUERY][:].bitcast(I32), 0)
        bias_rows = keep.tile([P, P], BF16, name="bias_rows")
        nc.vector.memset(bias_rows[:], 0.0)
        mask_sb = keep.tile([P, SEQ], BF16, name="mask_sb")
        nc.vector.memset(mask_sb[:], 1.0)
        scale_sb = keep.tile([P, 1], BF16, name="scale_sb")

        def load_bias(s):
            nc.sync.dma_start(
                out=bias_rows[SLICES * s : SLICES * (s + 1), :],
                in_=biases[s].rearrange("(j p) -> j p", p=P),
            )

        load_group(KEY, 0, 0)
        load_planes(KEY)
        load_codes(KEY)
        load_group(KEY, 0, 1)
        load_bias(KEY)
        load_bias(QUERY)
        load_group(QUERY, 0, 0)
        load_codes(QUERY)
        load_planes(QUERY)
        load_group(QUERY, 0, 1)
        nc.sync.dma_start(out=mask_sb[0:N_SEQ, :], in_=attention_mask)
        nc.sync.dma_start(out=scale_sb[:], in_=logit_scale.partition_broadcast(P))
        for c in range(1, N_CHUNKS):
            for s in (KEY, QUERY):
                load_chunk(s, c)

        last_window = N_SEQ - SEQ_PER_TILE
        selector = keep.tile([P, last_window + P], F32, name="selector")
        nc.vector.memset(selector[:], 0.0)
        for quarter in range(SEQ_PER_TILE):
            nc.vector.memset(
                selector[quarter * PAIRS : (quarter + 1) * PAIRS, last_window + quarter : last_window + quarter + 1],
                1.0,
            )
        scaled = keep.tile([P, N_SEQ + P], F32, name="scaled")
        nc.vector.memset(scaled[:], 0.0)
        exp_scale = keep.tile([P, 1], F32, name="exp_scale")
        table_probe = keep.tile([P, 1], F32, name="table_probe")
        nc.vector.memset(table_probe[:], 0.0)
        nc.scalar.activation(out=exp_scale[:], in_=table_probe[:], func=ACT.Exp)
        bias_cols = keep.tile([P, 2 * SLICES], F32, name="bias_cols")

        halves = [(s, c, e) for c in range(N_CHUNKS) for s in (KEY, QUERY) for e in range(2)]
        n_halves = len(halves)
        in_flight = {}

        def negated(n):
            s, c, e = halves[n]
            return c >= FIRST_PAIRED and e == 1

        def turn(n):
            s, c, e = halves[n]
            raw_words = raw[s][c][:].bitcast(F32)
            turned = psum_t.tile([P, TILES_PER_HALF, 2, P], F32, name="turned", tag="turned")
            for i in range(TILES_PER_HALF):
                for u in range(2):
                    nc.tensor.transpose(
                        turned[:, i, u, :],
                        raw_words[:, e, i, u : FEATURES // 2 : 2] if c == 0 else raw_words[:, i, e, u : FEATURES // 2 : 2],
                        ident_f32[:],
                    )
            grouped = stage.tile([P, HALF * PACK], BF16, name="grouped", align_bytes=64)
            grouped_view = grouped[:].bitcast(F32).rearrange("p (i r u) -> p i r u", i=TILES_PER_HALF, u=2)
            turned_view = turned[:].rearrange("p i u r -> p i r u")
            if n in VECTOR_TURNS:
                nc.vector.tensor_copy(out=grouped_view, in_=turned_view)
            else:
                nc.scalar.copy(out=grouped_view, in_=turned_view)
            in_flight[("grouped", n)] = grouped

        def quantise_states(n):
            x_codes = stage.tile([P, HALF], U32, name="x_codes", align_bytes=64)
            x_planes = stage.tile([P, HALF], U8, name="x_planes", align_bytes=64)
            nc.vector.quantize_mx(
                out=x_codes[:].bitcast(FP8X4), scales=x_planes[:], in_=in_flight[("grouped", n)][:]
            )
            in_flight[("x", n)] = (x_codes, x_planes)

        def project(n):
            s, c, e = halves[n]
            x_codes, x_planes = in_flight[("x", n)]
            if n in VECTOR_BIAS:
                accs = []
                for i in range(TILES_PER_HALF):
                    rows = slice(i * P, (i + 1) * P)
                    acc = psum_logits.tile([P, SLICES, P], F32, name="acc_v", tag="logits")
                    for j in range(SLICES):
                        nc.tensor.matmul_mx(
                            out=acc[:, j, :],
                            lhsT=w_codes[s][:, j * P : (j + 1) * P].bitcast(FP8X4),
                            lhsT_scale=w_planes[s][:, j * P : (j + 1) * P],
                            rhs=x_codes[:, rows].bitcast(FP8X4),
                            rhs_scale=x_planes[:, rows],
                            start=True,
                            stop=True,
                        )
                    accs.append(acc)
                in_flight[("accs", n)] = accs
                return
            by_slice = stage.tile([P, SLICES, HALF], BF16, name="by_slice")
            for pair in range(SLICES // 2):
                acc = psum_proj.tile([P, 2, HALF], F32, name="acc", tag="acc")
                for f in range(2):
                    cols = slice((2 * pair + f) * P, (2 * pair + f + 1) * P)
                    nc.tensor.matmul_mx(
                        out=acc[:, f, :],
                        lhsT=w_codes[s][:, cols].bitcast(FP8X4),
                        lhsT_scale=w_planes[s][:, cols],
                        rhs=x_codes[:].bitcast(FP8X4),
                        rhs_scale=x_planes[:],
                        start=True,
                        stop=True,
                    )
                for f in range(2):
                    j = 2 * pair + f
                    nc.scalar.activation(
                        out=by_slice[:, j, :],
                        in_=acc[:, f, :],
                        func=ACT.Identity,
                        bias=bias_cols[:, SLICES * s + j : SLICES * s + j + 1],
                    )
            in_flight[("by_slice", n)] = by_slice
            if negated(n):
                opposite = stage.tile([P, HALF * PACK], BF16, name="opposite", align_bytes=64)
                nc.scalar.mul(
                    out=opposite[:].rearrange("p (g i j) -> p g j i", i=4, j=SLICES),
                    in_=by_slice[:].rearrange("p j (g i) -> p g j i", i=4),
                    mul=-1.0,
                )
                in_flight[("opposite", n)] = opposite

        def regroup(n):
            s, c, e = halves[n]
            if n in VECTOR_BIAS:
                regrouped = stage.tile([P, HALF * PACK], BF16, name="regrouped_v", align_bytes=64)
                for i in range(TILES_PER_HALF):
                    nc.vector.tensor_tensor(
                        out=regrouped[:, i * P * PACK : (i + 1) * P * PACK].rearrange("p (r j) -> p r j", j=SLICES),
                        in0=in_flight[("accs", n)][i][:].rearrange("p j r -> p r j"),
                        in1=bias_cols[:, SLICES * s : SLICES * (s + 1)].unsqueeze(1).to_broadcast([P, P, SLICES]),
                        op=ALU.add,
                    )
                in_flight[("regrouped", n)] = regrouped
                return
            by_slice = in_flight[("by_slice", n)]
            regrouped = single.tile([P, HALF * PACK], BF16, name="regrouped", align_bytes=64)
            nc.gpsimd.tensor_scalar(
                out=regrouped[:].rearrange("p (r j) -> p r j", j=SLICES),
                in0=by_slice[:].rearrange("p j r -> p r j"),
                scalar1=1.0,
                scalar2=0.0,
                op0=ALU.mult,
                op1=ALU.add,
            )
            in_flight[("regrouped", n)] = regrouped

        def quantise_projected(n):
            s, c, e = halves[n]
            if negated(n):
                out_codes, out_planes = quantised(s, c, 2, 0, HALF)
                nc.vector.quantize_mx(
                    out=out_codes.bitcast(FP8X4), scales=out_planes, in_=in_flight[("opposite", n)][:]
                )
            if c == 0:
                for i in range(2):
                    out_codes, out_planes = quantised(s, c, i, e * P, P)
                    nc.vector.quantize_mx(
                        out=out_codes.bitcast(FP8X4),
                        scales=out_planes,
                        in_=in_flight[("regrouped", n)][:, i * P * PACK : (i + 1) * P * PACK],
                    )
                return
            out_codes, out_planes = quantised(s, c, e, 0, HALF)
            nc.vector.quantize_mx(
                out=out_codes.bitcast(FP8X4), scales=out_planes, in_=in_flight[("regrouped", n)][:]
            )

        def unlocked(n):
            s, c, e = halves[n]
            other_chunks = c if s == KEY else c + 1
            first = c * TILES_PER_CHUNK
            tiles = (first + e, first + e + 2) if c == 0 else (first + 2 * e, first + 2 * e + 1)
            new = [(s, t, o) for t in tiles for o in range(other_chunks)]
            if e == 1:
                new.extend([(1 - s, t, c) for t in range(other_chunks * TILES_PER_CHUNK)])
            return new

        def product(out, s, t, c, block, width, start, stop):
            chunk, place = divmod(t, TILES_PER_CHUNK)
            lhs_codes, lhs_planes = quantised(s, chunk, place // TILES_PER_HALF, place % TILES_PER_HALF * P, P)
            rhs_codes, rhs_planes = quantised(1 - s, c, block, 0, width)
            nc.tensor.matmul_mx(
                out=out,
                lhsT=lhs_codes.bitcast(FP8X4),
                lhsT_scale=lhs_planes,
                rhs=rhs_codes.bitcast(FP8X4),
                rhs_scale=rhs_planes,
                start=start,
                stop=stop,
            )

        filled = {}
        clock = [0]

        def note_maxima(s, t, n_sequences):
            filled[(s, t)] = [filled.get((s, t), [0, 0])[0] + n_sequences, clock[0]]

        def score(s, t, c):
            logits = psum_logits.tile([P, CHUNK], F32, name="logits")
            if c < FIRST_PAIRED:
                product(logits[:], s, t, c, 0, CHUNK, True, True)
            else:
                for e in range(2):
                    product(logits[:, e * HALF : (e + 1) * HALF], s, t, c, e, HALF, True, True)
            nc.vector.tensor_reduce(
                out=maxima[t][:, s, c * SEQ_PER_CHUNK : (c + 1) * SEQ_PER_CHUNK],
                in_=logits[:].rearrange("p (e b m) -> p b e m", e=2, m=PAIRS),
                axis=AXIS_XY,
                op=ALU.max,
            )
            note_maxima(s, t, SEQ_PER_CHUNK)

        units = []
        begun = []
        summed = []
        gate = [False]

        def unit_begin(s, t):
            difference = psum_t.tile([P, CHUNK], F32, name="difference", tag="turned")
            odd = psum_proj.tile([P, CHUNK], F32, name="odd", tag="acc")
            product(difference[:], s, t, FIRST_PAIRED, 0, CHUNK, True, False)
            product(difference[:], s, t, FIRST_PAIRED, 2, CHUNK, False, True)
            product(odd[:], s, t, FIRST_PAIRED, 1, CHUNK, True, True)
            larger = halving.tile([P, CHUNK], F32, name="larger")
            nc.scalar.activation(out=larger[:], in_=difference[:], func=ACT.Relu)
            odd_sb = halving.tile([P, CHUNK], F32, name="odd_sb")
            nc.scalar.copy(out=odd_sb[:], in_=odd[:])
            units.append((s, t, larger, odd_sb))
            begun.append(clock[0])

        def unit_middle(k):
            s, t, larger, odd_sb = units[k]
            total = larger
            if k == 0:
                total = single.tile([P, CHUNK], F32, name="first_total", tag="regrouped", align_bytes=64)
                units[k] = (s, t, total, odd_sb)
            nc.gpsimd.tensor_tensor(out=total[:], in0=larger[:], in1=odd_sb[:], op=ALU.add)
            summed.append(clock[0])

        def unit_end(k):
            s, t, larger, odd_sb = units[k]
            nc.vector.tensor_reduce(
                out=maxima[t][:, s, FIRST_PAIRED * SEQ_PER_CHUNK : N_SEQ],
                in_=larger[:].rearrange("p (b m) -> p b m", m=PAIRS),
                axis=AXIS_X,
                op=ALU.max,
            )
            note_maxima(s, t, (N_CHUNKS - FIRST_PAIRED) * SEQ_PER_CHUNK)

        added = []
        sums_of = {}

        def add_up(t):
            if len(added) == 0:
                sums_of[0] = psum_logits.tile([P, 2 * N_SEQ], F32, name="sums", tag="logits")
            first_seq = (t // TILES_PER_CHUNK) * SEQ_PER_CHUNK + (t % TILES_PER_HALF) * SEQ_PER_TILE
            window = last_window - first_seq
            nc.tensor.matmul(
                out=sums_of[0][:],
                lhsT=selector[:, window : window + P],
                rhs=maxima[t][:].rearrange("p s b -> p (s b)"),
                start=(len(added) == 0),
                stop=(len(added) == N_TILES - 1),
            )
            added.append(t)

        waiting = []
        paired = []
        n_scored = [0, 0]

        def score_waiting(n_products):
            for unit in waiting[n_scored[0] : n_scored[0] + n_products]:
                score(*unit)
            n_scored[0] = min(n_scored[0] + n_products, len(waiting))

        def step():
            clock[0] += 1
            due = (clock[0] * ALONE_PER_STEPS[0]) // ALONE_PER_STEPS[1] - n_scored[1]
            before = n_scored[0]
            score_waiting(1)
            if len(units) < len(paired):
                unit_begin(*paired[len(units)])
            score_waiting(due - 1)
            n_scored[1] += n_scored[0] - before
            if gate[0] and len(summed) < len(units) and begun[len(summed)] < clock[0]:
                unit_middle(len(summed))
            for k in range(len(summed)):
                if summed[k] + LAG - 1 == clock[0]:
                    unit_end(k)
            for t in range(N_TILES):
                if t not in added and all(
                    filled.get((s, t), [0, 0])[0] == N_SEQ and filled[(s, t)][1] + SUM_LAG <= clock[0]
                    for s in (QUERY, KEY)
                ):
                    add_up(t)

        def warm_up(n_matmuls):
            for k in range(n_matmuls):
                idle = psum_proj.tile([P, CHUNK], F32, name="idle", tag="acc")
                nc.tensor.matmul(out=idle[:], lhsT=zeros[:, 0:P], rhs=zeros[:], start=True, stop=True)

        mask_sum = keep.tile([P, 1], F32, name="mask_sum")
        inv_mask_sum = keep.tile([P, 1], F32, name="inv_mask_sum")
        factors = keep.tile([P, 2, N_SEQ], F32, name="factors")

        def make_factors():
            nc.vector.tensor_reduce(out=mask_sum[:], in_=mask_sb[:], axis=AXIS_X, op=ALU.add)
            nc.vector.reciprocal(out=inv_mask_sum[:], in_=mask_sum[:])
            nc.vector.tensor_scalar(
                out=factors[:, QUERY, :],
                in0=exp_scale[:].to_broadcast([P, N_SEQ]),
                scalar1=inv_mask_sum[:, 0:1],
                scalar2=0.5,
                op0=ALU.mult,
                op1=ALU.mult,
            )
            nc.vector.tensor_scalar(
                out=factors[:, KEY, :],
                in0=exp_scale[:].to_broadcast([P, N_SEQ]),
                scalar1=0.5 / SEQ,
                scalar2=None,
                op0=ALU.mult,
            )

        late = []

        def finish(n):
            quantise_projected(n)
            for unit in unlocked(n):
                if unit[2] < FIRST_PAIRED:
                    waiting.append(unit)
                elif unit[2] == N_CHUNKS - 1:
                    late.append((unit[0], unit[1]))

        n_released = [0]

        def release():
            for pair in late[n_released[0] :]:
                n_released[0] += 1
                if n_released[0] % DIRECT_EVERY == 0:
                    waiting.extend([(pair[0], pair[1], c) for c in range(FIRST_PAIRED, N_CHUNKS)])
                else:
                    paired.append(pair)

        def score_some():
            score_waiting(min(PER_SLOT, max(len(waiting) - n_scored[0] - HELD_BACK, 0)))

        warm_up(4)
        turn(0)
        warm_up(2)
        turn(1)
        quantise_states(0)
        bias_t = psum_t.tile([P, P], BF16, name="bias_t", tag="turned")
        nc.tensor.transpose(bias_t[:], bias_rows[:], ident_bf16[:])
        nc.vector.tensor_copy(out=bias_cols[:], in_=bias_t[:, 0 : 2 * SLICES])
        project(0)
        turn(2)
        quantise_states(1)
        project(1)
        regroup(0)
        quantise_states(2)
        turn(3)
        finish(0)
        project(2)
        regroup(1)
        quantise_states(3)
        turn(4)
        nc.scalar.activation(out=exp_scale[:], in_=scale_sb[:], func=ACT.Exp)
        regroup(2)
        project(3)
        finish(1)
        finish(2)
        quantise_states(4)
        score_some()
        regroup(3)
        turn(5)
        project(4)
        make_factors()
        turn(6)
        finish(3)
        regroup(4)
        quantise_states(5)
        score_some()
        project(5)
        turn(7)
        quantise_states(6)

        for n in range(4, n_halves):
            if n + 4 < n_halves and n < PAIRED_TURNS:
                turn(n + 4)
            elif n + 4 < n_halves and n % 2 == 0:
                turn(n + 4)
                turn(n + 5)
            if n + 3 < n_halves:
                quantise_states(n + 3)
            finish(n)
            if n + 1 < n_halves:
                regroup(n + 1)
            if n + 2 < n_halves:
                project(n + 2)
            if n < n_halves - EARLY_SLOTS:
                score_some()
            elif n + 1 < n_halves:
                release()
                for k in range(STEPS_PER_SLOT):
                    step()

        gate[0] = True
        release()
        while len(added) < N_TILES:
            step()
        sums = sums_of[0]

        nc.vector.tensor_tensor(
            out=scaled[:, 0 : 2 * N_SEQ],
            in0=sums[:],
            in1=factors[:].rearrange("p s b -> p (s b)"),
            op=ALU.mult,
        )
        flipped = psum_t.tile([P, 2, P], F32, name="flipped", tag="turned")
        nc.tensor.transpose(flipped[:, QUERY, :], scaled[:, N_SEQ : N_SEQ + P], ident_f32[:])
        nc.tensor.transpose(flipped[:, KEY, :], scaled[:, 0:P], ident_f32[:])
        result = keep.tile([P, 2, N_SEQ], F32, name="result")
        nc.vector.tensor_tensor(
            out=result[:],
            in0=scaled[:, 0 : 2 * N_SEQ].rearrange("p (s b) -> p s b", s=2),
            in1=flipped[:, :, 0:N_SEQ],
            op=ALU.add,
        )
        nc.sync.dma_start(out=out_0, in_=result[0:N_SEQ, QUERY, :])
        nc.sync.dma_start(out=out_1, in_=result[0:N_SEQ, KEY, :])
